import numpy as np
import ml_dtypes


def mxq(x, axis, fmt="e4m3"):
    dtype, down = {"e4m3": (ml_dtypes.float8_e4m3fn, 7), "e5m2": (ml_dtypes.float8_e5m2, 14)}[fmt]
    v = np.moveaxis(np.asarray(x, np.float32).astype(ml_dtypes.bfloat16).astype(np.float64), axis, -1)
    blocks = v.reshape(v.shape[:-1] + (-1, 32))
    amax = np.abs(blocks).max(-1, keepdims=True)
    byte = np.maximum(np.where(amax > 0, np.frexp(amax)[1] - 1 + 127, 0) - down, 1)
    scale = np.exp2(byte - 127.0)
    codes = (blocks / scale).astype(np.float32).astype(dtype).astype(np.float64)
    return np.moveaxis((codes * scale).reshape(v.shape), -1, axis)


WIDE = False


def mx_kscale(k):
    if not WIDE:
        return np.ones(k)
    levels = np.array([10, -10, 5, -5, 0])
    a = np.random.permutation(np.resize(levels, k // 512 * 4)).reshape(k // 512, 4)
    idx = np.arange(k)
    return np.exp2(a[idx // 512, idx % 128 // 32])


BF16 = ml_dtypes.bfloat16


def bf(x):
    return np.asarray(x, np.float32).astype(BF16)


def f64(x):
    return np.asarray(x).astype(np.float64)


B, C, M, NX, NY = 1, 8, 1024, 256, 512


def setup_inputs():
    s = mx_kscale(M)
    return {
        "kspace_real": bf(np.random.standard_normal((B, C, M)) * 2.0 / np.sqrt(M) * s),
        "kspace_imag": bf(np.random.standard_normal((B, C, M)) * 2.0 / np.sqrt(M) * s),
        "trajectory": bf((np.random.random((2, M)) - 0.5) * (2.0 * np.pi)),
        "smaps_real": bf(np.random.standard_normal((B, C, NX, NY)) / np.sqrt(C)),
        "smaps_imag": bf(np.random.standard_normal((B, C, NX, NY)) / np.sqrt(C)),
        "density_comp": bf(np.random.random(M) / s),
    }


def reference(kspace_real, kspace_imag, trajectory, smaps_real, smaps_imag, density_comp):
    kr, ki, w = f64(kspace_real), f64(kspace_imag), f64(density_comp)
    traj = f64(trajectory).T
    gx = np.arange(NX, dtype=np.float64) - NX // 2
    yy = np.arange(NY, dtype=np.float64)
    ax = traj[:, 0:1] * gx[None, :] - traj[:, 1:2] * (NY // 2)
    ay = traj[:, 1:2] * yy[None, :]
    exr, exi = np.cos(ax).T[None, None], np.sin(ax).T[None, None]
    eyr, eyi = np.cos(ay), np.sin(ay)
    ar = kr[:, :, None, :] * exr - ki[:, :, None, :] * exi
    ai = kr[:, :, None, :] * exi + ki[:, :, None, :] * exr
    er = w[:, None] * eyr
    ei = w[:, None] * eyi
    arq = mxq(ar, 3, "e4m3")
    aiq = mxq(ai, 3, "e4m3")
    erq = mxq(er, 0, "e4m3")
    eiq = mxq(ei, 0, "e4m3")
    rr = (arq @ erq) - (aiq @ eiq)
    ri = (arq @ eiq) + (aiq @ erq)
    sr, si = f64(smaps_real), f64(smaps_imag)
    cr = np.sum(rr * sr + ri * si, axis=1)
    ci = np.sum(ri * sr - rr * si, axis=1)
    return np.sqrt(cr ** 2 + ci ** 2)[..., None]

@@ -1,0 +1,301 @@
+import math
+
+import concourse.mybir as mybir
+from concourse.masks import make_identity
+
+F32 = mybir.dt.float32
+BF16 = mybir.dt.bfloat16
+U8 = mybir.dt.uint8
+U32 = mybir.dt.uint32
+FP8X4 = mybir.dt.float8_e4m3fn_x4
+ALU = mybir.AluOpType
+ACT = mybir.ActivationFunctionType
+
+P = 128
+PACK = 4
+K_PASS = P * PACK
+
+COILS, SAMPLES, NX, NY = 8, 1024, 256, 512
+PASSES = SAMPLES // K_PASS
+PLANES = PASSES * PACK
+X_TILES = NX // P
+FINE = 64
+X_COARSE = NX // FINE
+Y_COARSE = NY // FINE
+
+TWO_PI = 2.0 * math.pi
+TWO_PI_HIGH = round(TWO_PI * 4096.0) / 4096.0
+TWO_PI_LOW = TWO_PI - TWO_PI_HIGH
+ROUNDER = 1.5 * 2.0**23
+
+E_RE, E_IM, E_IM_NEG = 0, 1, 2
+
+FLOPS = 4 * 2 * COILS * NX * SAMPLES * NY
+
+
+def by_plane(vector_ap, lead):
+    return vector_ap.rearrange(lead + " (g p t) -> p " + lead + " g t", g=PASSES, p=P, t=PACK)
+
+
+def wrap(nc, pool, angle, shape, turn_shift, label):
+    turns = pool.tile(shape, F32, name="turns_" + label)
+    nc.vector.tensor_scalar(
+        out=turns[:], in0=angle, scalar1=1.0 / TWO_PI, scalar2=turn_shift, op0=ALU.mult, op1=ALU.add
+    )
+    nc.vector.tensor_scalar(
+        out=turns[:], in0=turns[:], scalar1=ROUNDER, scalar2=ROUNDER, op0=ALU.add, op1=ALU.subtract
+    )
+    wrapped = pool.tile(shape, F32, name="wrapped_" + label)
+    nc.vector.scalar_tensor_tensor(
+        out=wrapped[:], in0=turns[:], scalar=-TWO_PI_HIGH, in1=angle, op0=ALU.mult, op1=ALU.add
+    )
+    nc.vector.scalar_tensor_tensor(
+        out=wrapped[:], in0=turns[:], scalar=-TWO_PI_LOW, in1=wrapped[:], op0=ALU.mult, op1=ALU.add
+    )
+    return wrapped
+
+
+def angle_tables(nc, pool, rate, steps, starts, n_coarse, phase, label):
+    fine_shape = [P, PLANES, FINE]
+    fine_angle = pool.tile(fine_shape, F32, name="fine_angle_" + label)
+    nc.vector.tensor_tensor(
+        out=fine_angle[:],
+        in0=rate.unsqueeze(2).to_broadcast(fine_shape),
+        in1=steps.unsqueeze(1).to_broadcast(fine_shape),
+        op=ALU.mult,
+    )
+    fine = wrap(nc, pool, fine_angle[:], fine_shape, 0.0, "fine_" + label)
+
+    coarse_shape = [P, PLANES, n_coarse]
+    coarse_angle = pool.tile(coarse_shape, F32, name="coarse_angle_" + label)
+    nc.vector.tensor_tensor(
+        out=coarse_angle[:],
+        in0=rate.unsqueeze(2).to_broadcast(coarse_shape),
+        in1=starts.unsqueeze(1).to_broadcast(coarse_shape),
+        op=ALU.mult,
+    )
+    if phase is not None:
+        nc.vector.tensor_tensor(
+            out=coarse_angle[:],
+            in0=coarse_angle[:],
+            in1=phase.unsqueeze(2).to_broadcast(coarse_shape),
+            op=ALU.subtract,
+        )
+    for_cos = wrap(nc, pool, coarse_angle[:], coarse_shape, 0.0, "cos_" + label)
+    half_cos = pool.tile(coarse_shape, F32, name="half_cos_" + label)
+    nc.vector.tensor_scalar(
+        out=half_cos[:], in0=for_cos[:], scalar1=0.5, scalar2=None, op0=ALU.mult
+    )
+    for_sin = wrap(nc, pool, coarse_angle[:], coarse_shape, -0.25, "sin_" + label)
+    half_sin = pool.tile(coarse_shape, F32, name="half_sin_" + label)
+    nc.vector.tensor_scalar(
+        out=half_sin[:], in0=for_sin[:], scalar1=-0.5 * math.pi, scalar2=0.5, op0=ALU.add, op1=ALU.mult
+    )
+    return fine, half_cos, half_sin
+
+
+def half_angle_sines(nc, out, fine, half_cos, half_sin, plane, n_coarse):
+    for which, half in enumerate((half_cos, half_sin)):
+        for coarse in range(n_coarse):
+            nc.scalar.activation(
+                out=out[:, which, coarse * FINE : (coarse + 1) * FINE],
+                in_=fine[:, plane, :],
+                func=ACT.Sin,
+                bias=half[:, plane, coarse : coarse + 1],
+                scale=0.5,
+            )
+
+
+def quantise(nc, grouped, codes, scales):
+    nc.vector.quantize_mx(
+        out=codes.bitcast(FP8X4), scales=scales, in_=grouped.rearrange("p w t -> p (w t)")
+    )
+
+
+def tile_adjoint_kernel(
+    tc, kspace_real, kspace_imag, trajectory, smaps_real, smaps_imag, density_comp, out
+):
+    nc = tc.nc
+    with (
+        tc.tile_pool(name="keep", bufs=1) as keep,
+        tc.tile_pool(name="tables", bufs=1) as tables,
+        tc.tile_pool(name="stream", bufs=3) as stream,
+        tc.tile_pool(name="coil", bufs=4) as coil_pool,
+        tc.tile_pool(name="ending", bufs=1) as ending,
+        tc.psum_pool(name="sums", bufs=1) as sums,
+        tc.psum_pool(name="recon", bufs=2) as recon,
+    ):
+        traj_bf = keep.tile([P, 2, PASSES, PACK], BF16)
+        nc.sync.dma_start(out=traj_bf[:], in_=by_plane(trajectory, "a"))
+        k_re_bf = keep.tile([P, COILS, PASSES, PACK], BF16)
+        nc.sync.dma_start(out=k_re_bf[:], in_=by_plane(kspace_real.rearrange("b c m -> (b c) m"), "c"))
+        k_im_bf = keep.tile([P, COILS, PASSES, PACK], BF16)
+        nc.sync.dma_start(out=k_im_bf[:], in_=by_plane(kspace_imag.rearrange("b c m -> (b c) m"), "c"))
+        density_bf = keep.tile([P, 1, PASSES, PACK], BF16)
+        nc.sync.dma_start(out=density_bf[:], in_=by_plane(density_comp.rearrange("(o m) -> o m", o=1), "o"))
+
+        maps_re = keep.tile([P, COILS, X_TILES, NY], BF16)
+        maps_im = keep.tile([P, COILS, X_TILES, NY], BF16)
+        maps_re_dram = smaps_real.rearrange("b c (h p) y -> p (b c) h y", p=P)
+        maps_im_dram = smaps_imag.rearrange("b c (h p) y -> p (b c) h y", p=P)
+        for c in range(COILS):
+            nc.sync.dma_start(out=maps_re[:, c], in_=maps_re_dram[:, c])
+            nc.sync.dma_start(out=maps_im[:, c], in_=maps_im_dram[:, c])
+
+        steps = keep.tile([P, FINE], F32)
+        nc.gpsimd.iota(
+            out=steps[:], pattern=[[1, FINE]], base=0, channel_multiplier=0,
+            allow_small_or_imprecise_dtypes=True,
+        )
+        x_starts = keep.tile([P, X_COARSE], F32)
+        nc.gpsimd.iota(
+            out=x_starts[:], pattern=[[FINE, X_COARSE]], base=-(NX // 2), channel_multiplier=0,
+            allow_small_or_imprecise_dtypes=True,
+        )
+        y_starts = keep.tile([P, Y_COARSE], F32)
+        nc.gpsimd.iota(
+            out=y_starts[:], pattern=[[FINE, Y_COARSE]], base=0, channel_multiplier=0,
+            allow_small_or_imprecise_dtypes=True,
+        )
+        identity = keep.tile([P, P], F32)
+        make_identity(nc, identity[:])
+
+        traj = keep.tile([P, 2, PLANES], F32)
+        nc.vector.tensor_copy(out=traj[:], in_=traj_bf[:].rearrange("p a g t -> p a (g t)"))
+        kx, ky = traj[:, 0, :], traj[:, 1, :]
+        centring = keep.tile([P, PLANES], F32)
+        nc.vector.tensor_scalar(
+            out=centring[:], in0=ky, scalar1=float(NY // 2), scalar2=None, op0=ALU.mult
+        )
+
+        fine_x, half_cos_x, half_sin_x = angle_tables(
+            nc, tables, kx, steps[:], x_starts[:], X_COARSE, centring[:], "x"
+        )
+        q_x = keep.tile([P, PLANES, 3 * NX], F32)
+        for plane in range(PLANES):
+            sines_x = stream.tile([P, 2, NX], F32)
+            half_angle_sines(nc, sines_x, fine_x, half_cos_x, half_sin_x, plane, X_COARSE)
+            flat = sines_x[:].rearrange("p w x -> p (w x)")
+            nc.vector.tensor_tensor(out=q_x[:, plane, 0 : 2 * NX], in0=flat, in1=flat, op=ALU.mult)
+            nc.vector.tensor_scalar(
+                out=q_x[:, plane, 2 * NX : 3 * NX], in0=q_x[:, plane, 0:NX],
+                scalar1=-1.0, scalar2=1.0, op0=ALU.mult, op1=ALU.add,
+            )
+
+        k_shape = [P, COILS, PLANES]
+        k_re_flat = k_re_bf[:].rearrange("p c g t -> p c (g t)")
+        k_im_flat = k_im_bf[:].rearrange("p c g t -> p c (g t)")
+        k_difference = keep.tile(k_shape, F32)
+        nc.vector.tensor_tensor(out=k_difference[:], in0=k_re_flat, in1=k_im_flat, op=ALU.subtract)
+        k_re_minus2 = keep.tile(k_shape, F32)
+        nc.vector.tensor_scalar(out=k_re_minus2[:], in0=k_re_flat, scalar1=-2.0, scalar2=None, op0=ALU.mult)
+        k_im_plus2 = keep.tile(k_shape, F32)
+        nc.vector.tensor_scalar(out=k_im_plus2[:], in0=k_im_flat, scalar1=2.0, scalar2=None, op0=ALU.mult)
+
+        def quantised_a(c):
+            a_codes = coil_pool.tile([P, PASSES, 2, NX], U32, align_bytes=64)
+            a_scales = coil_pool.tile([P, PASSES, 2, NX], U8, align_bytes=64)
+            for g in range(PASSES):
+                a_planes = stream.tile([P, PACK, 2 * NX], BF16)
+                for t in range(PACK):
+                    plane = g * PACK + t
+                    first_terms = stream.tile([P, 2 * NX], F32)
+                    nc.scalar.activation(
+                        out=first_terms[:], in_=q_x[:, plane, 0 : 2 * NX], func=ACT.Identity,
+                        bias=k_difference[:, c, plane : plane + 1],
+                        scale=k_re_minus2[:, c, plane : plane + 1],
+                    )
+                    nc.vector.scalar_tensor_tensor(
+                        out=a_planes[:, t, :], in0=q_x[:, plane, NX : 3 * NX],
+                        scalar=k_im_plus2[:, c, plane : plane + 1], in1=first_terms[:],
+                        op0=ALU.mult, op1=ALU.add,
+                    )
+                a_grouped = stream.tile([P, 2 * NX, PACK], BF16, align_bytes=64)
+                nc.vector.tensor_copy(out=a_grouped[:], in_=a_planes[:].rearrange("p t w -> p w t"))
+                quantise(
+                    nc, a_grouped[:],
+                    a_codes[:, g].rearrange("p w x -> p (w x)"),
+                    a_scales[:, g].rearrange("p w x -> p (w x)"),
+                )
+            return a_codes, a_scales
+
+        next_a = quantised_a(0)
+
+        density = keep.tile([P, PLANES], F32)
+        nc.vector.tensor_copy(out=density[:], in_=density_bf[:].rearrange("p o g t -> p (o g t)"))
+        density_minus2 = keep.tile([P, PLANES], F32)
+        nc.vector.tensor_scalar(out=density_minus2[:], in0=density[:], scalar1=-2.0, scalar2=None, op0=ALU.mult)
+        fine_y, half_cos_y, half_sin_y = angle_tables(
+            nc, tables, ky, steps[:], y_starts[:], Y_COARSE, None, "y"
+        )
+        e_codes = keep.tile([P, PASSES, 3, NY], U32, align_bytes=64)
+        e_scales = keep.tile([P, PASSES, 3, NY], U8, align_bytes=64)
+        for g in range(PASSES):
+            e_planes = stream.tile([P, PACK, 2, NY], BF16, bufs=2)
+            for t in range(PACK):
+                plane = g * PACK + t
+                sines_y = stream.tile([P, 2, NY], F32)
+                half_angle_sines(nc, sines_y, fine_y, half_cos_y, half_sin_y, plane, Y_COARSE)
+                nc.scalar.activation(out=sines_y[:], in_=sines_y[:], func=ACT.Square)
+                nc.scalar.activation(
+                    out=e_planes[:, t], in_=sines_y[:], func=ACT.Identity,
+                    bias=density[:, plane : plane + 1], scale=density_minus2[:, plane : plane + 1],
+                )
+            nc.vector.memset(e_planes[:, :, 1, 0:1], 0.0)
+            for kind, which, sign in ((E_RE, 0, 1.0), (E_IM, 1, 1.0), (E_IM_NEG, 1, -1.0)):
+                e_grouped = stream.tile([P, NY, PACK], BF16, align_bytes=64)
+                nc.vector.tensor_scalar(
+                    out=e_grouped[:], in0=e_planes[:, :, which, :].rearrange("p t y -> p y t"),
+                    scalar1=sign, scalar2=None, op0=ALU.mult,
+                )
+                quantise(nc, e_grouped[:], e_codes[:, g, kind, :], e_scales[:, g, kind, :])
+
+        combined_re = [sums.tile([P, NY], F32, name="combined_re_%d" % h) for h in range(X_TILES)]
+        combined_im = [sums.tile([P, NY], F32, name="combined_im_%d" % h) for h in range(X_TILES)]
+        for c in range(COILS):
+            a_codes, a_scales = next_a
+            if c + 1 < COILS:
+                next_a = quantised_a(c + 1)
+            for h in range(X_TILES):
+                x_cols = slice(h * P, (h + 1) * P)
+                recon_re = recon.tile([P, NY], F32)
+                recon_im = recon.tile([P, NY], F32)
+                for g in range(PASSES):
+                    for part, kind_for_re, kind_for_im in ((0, E_RE, E_IM), (1, E_IM_NEG, E_RE)):
+                        for acc, kind in ((recon_re, kind_for_re), (recon_im, kind_for_im)):
+                            nc.tensor.matmul_mx(
+                                out=acc[:],
+                                lhsT=a_codes[:, g, part, x_cols].bitcast(FP8X4),
+                                lhsT_scale=a_scales[:, g, part, x_cols],
+                                rhs=e_codes[:, g, kind, :].bitcast(FP8X4),
+                                rhs_scale=e_scales[:, g, kind, :],
+                                start=(g == 0 and part == 0),
+                                stop=(g == PASSES - 1 and part == 1),
+                            )
+                s_re, s_im = maps_re[:, c, h, :], maps_im[:, c, h, :]
+                re_s_re = stream.tile([P, NY], F32)
+                nc.vector.tensor_tensor(out=re_s_re[:], in0=recon_re[:], in1=s_re, op=ALU.mult)
+                im_s_im = stream.tile([P, NY], F32)
+                nc.vector.tensor_tensor(out=im_s_im[:], in0=recon_im[:], in1=s_im, op=ALU.mult)
+                im_s_re = stream.tile([P, NY], F32)
+                nc.vector.tensor_tensor(out=im_s_re[:], in0=recon_im[:], in1=s_re, op=ALU.mult)
+                re_s_im = stream.tile([P, NY], F32)
+                nc.vector.tensor_tensor(out=re_s_im[:], in0=recon_re[:], in1=s_im, op=ALU.mult)
+                im_term = stream.tile([P, NY], F32)
+                nc.gpsimd.tensor_tensor(out=im_term[:], in0=im_s_re[:], in1=re_s_im[:], op=ALU.subtract)
+                first_coil, last_coil = c == 0, c == COILS - 1
+                nc.tensor.matmul(out=combined_re[h][:], lhsT=identity[:], rhs=re_s_re[:], start=first_coil, stop=False)
+                nc.tensor.matmul(out=combined_re[h][:], lhsT=identity[:], rhs=im_s_im[:], start=False, stop=last_coil)
+                nc.tensor.matmul(out=combined_im[h][:], lhsT=identity[:], rhs=im_term[:], start=first_coil, stop=last_coil)
+
+        out_rows = out.rearrange("b x y o -> (b x) (y o)")
+        for h in range(X_TILES):
+            re_squared = ending.tile([P, NY], F32)
+            nc.scalar.activation(out=re_squared[:], in_=combined_re[h][:], func=ACT.Square)
+            im_squared = ending.tile([P, NY], F32)
+            nc.scalar.activation(out=im_squared[:], in_=combined_im[h][:], func=ACT.Square)
+            power = ending.tile([P, NY], F32)
+            nc.vector.tensor_tensor(out=power[:], in0=re_squared[:], in1=im_squared[:], op=ALU.add)
+            magnitude = ending.tile([P, NY], F32)
+            nc.scalar.activation(out=magnitude[:], in_=power[:], func=ACT.Sqrt)
+            nc.sync.dma_start(out=out_rows[h * P : (h + 1) * P, :], in_=magnitude[:])

@@ -20,6 +20,7 @@ PASSES = SAMPLES // K_PASS
 PLANES = PASSES * PACK
 X_TILES = NX // P
 FINE = 64
+RUN = 4
 X_COARSE = NX // FINE
 Y_COARSE = NY // FINE
 
@@ -37,73 +38,45 @@ def by_plane(vector_ap, lead):
     return vector_ap.rearrange(lead + " (g p t) -> p " + lead + " g t", g=PASSES, p=P, t=PACK)
 
 
-def wrap(nc, pool, angle, shape, turn_shift, label):
-    turns = pool.tile(shape, F32, name="turns_" + label)
-    nc.vector.tensor_scalar(
-        out=turns[:], in0=angle, scalar1=1.0 / TWO_PI, scalar2=turn_shift, op0=ALU.mult, op1=ALU.add
-    )
-    nc.vector.tensor_scalar(
-        out=turns[:], in0=turns[:], scalar1=ROUNDER, scalar2=ROUNDER, op0=ALU.add, op1=ALU.subtract
-    )
-    wrapped = pool.tile(shape, F32, name="wrapped_" + label)
-    nc.vector.scalar_tensor_tensor(
-        out=wrapped[:], in0=turns[:], scalar=-TWO_PI_HIGH, in1=angle, op0=ALU.mult, op1=ALU.add
-    )
-    nc.vector.scalar_tensor_tensor(
-        out=wrapped[:], in0=turns[:], scalar=-TWO_PI_LOW, in1=wrapped[:], op0=ALU.mult, op1=ALU.add
-    )
+def wrap_all(nc, pool, jobs):
+    turns = [pool.tile(shape, F32, name="turns_" + label) for angle, shape, turn_shift, label in jobs]
+    wrapped = [pool.tile(shape, F32, name="wrapped_" + label) for angle, shape, turn_shift, label in jobs]
+    for i, (angle, shape, turn_shift, label) in enumerate(jobs):
+        nc.vector.tensor_scalar(
+            out=turns[i][:], in0=angle, scalar1=1.0 / TWO_PI, scalar2=turn_shift, op0=ALU.mult, op1=ALU.add
+        )
+    for i in range(len(jobs)):
+        nc.vector.tensor_scalar(
+            out=turns[i][:], in0=turns[i][:], scalar1=ROUNDER, scalar2=ROUNDER, op0=ALU.add, op1=ALU.subtract
+        )
+    for i, (angle, shape, turn_shift, label) in enumerate(jobs):
+        nc.vector.scalar_tensor_tensor(
+            out=wrapped[i][:], in0=turns[i][:], scalar=-TWO_PI_HIGH, in1=angle, op0=ALU.mult, op1=ALU.add
+        )
+    for i in range(len(jobs)):
+        nc.vector.scalar_tensor_tensor(
+            out=wrapped[i][:], in0=turns[i][:], scalar=-TWO_PI_LOW, in1=wrapped[i][:], op0=ALU.mult, op1=ALU.add
+        )
     return wrapped
 
 
-def angle_tables(nc, pool, rate, steps, starts, n_coarse, phase, label):
-    fine_shape = [P, PLANES, FINE]
-    fine_angle = pool.tile(fine_shape, F32, name="fine_angle_" + label)
-    nc.vector.tensor_tensor(
-        out=fine_angle[:],
-        in0=rate.unsqueeze(2).to_broadcast(fine_shape),
-        in1=steps.unsqueeze(1).to_broadcast(fine_shape),
-        op=ALU.mult,
-    )
-    fine = wrap(nc, pool, fine_angle[:], fine_shape, 0.0, "fine_" + label)
-
-    coarse_shape = [P, PLANES, n_coarse]
-    coarse_angle = pool.tile(coarse_shape, F32, name="coarse_angle_" + label)
-    nc.vector.tensor_tensor(
-        out=coarse_angle[:],
-        in0=rate.unsqueeze(2).to_broadcast(coarse_shape),
-        in1=starts.unsqueeze(1).to_broadcast(coarse_shape),
-        op=ALU.mult,
-    )
-    if phase is not None:
-        nc.vector.tensor_tensor(
-            out=coarse_angle[:],
-            in0=coarse_angle[:],
-            in1=phase.unsqueeze(2).to_broadcast(coarse_shape),
-            op=ALU.subtract,
-        )
-    for_cos = wrap(nc, pool, coarse_angle[:], coarse_shape, 0.0, "cos_" + label)
-    half_cos = pool.tile(coarse_shape, F32, name="half_cos_" + label)
-    nc.vector.tensor_scalar(
-        out=half_cos[:], in0=for_cos[:], scalar1=0.5, scalar2=None, op0=ALU.mult
-    )
-    for_sin = wrap(nc, pool, coarse_angle[:], coarse_shape, -0.25, "sin_" + label)
-    half_sin = pool.tile(coarse_shape, F32, name="half_sin_" + label)
-    nc.vector.tensor_scalar(
-        out=half_sin[:], in0=for_sin[:], scalar1=-0.5 * math.pi, scalar2=0.5, op0=ALU.add, op1=ALU.mult
-    )
-    return fine, half_cos, half_sin
-
-
-def half_angle_sines(nc, out, fine, half_cos, half_sin, plane, n_coarse):
+def half_angle_sines(nc, out, fine, half_cos, half_sin, n_coarse):
     for which, half in enumerate((half_cos, half_sin)):
         for coarse in range(n_coarse):
             nc.scalar.activation(
                 out=out[:, which, coarse * FINE : (coarse + 1) * FINE],
-                in_=fine[:, plane, :],
+                in_=fine,
                 func=ACT.Sin,
-                bias=half[:, plane, coarse : coarse + 1],
+                bias=half[:, coarse : coarse + 1],
                 scale=0.5,
             )
+
+
+def side_by_side(grouped, planes):
+    return (
+        grouped.rearrange("p (w i) t -> p w t i", i=RUN),
+        planes.rearrange("p t (w i) -> p w t i", i=RUN),
+    )
 
 
 def quantise(nc, grouped, codes, scales):
@@ -147,14 +120,13 @@ def tile_adjoint_kernel(
             out=steps[:], pattern=[[1, FINE]], base=0, channel_multiplier=0,
             allow_small_or_imprecise_dtypes=True,
         )
-        x_starts = keep.tile([P, X_COARSE], F32)
+        starts = keep.tile([P, X_COARSE + Y_COARSE], F32)
         nc.gpsimd.iota(
-            out=x_starts[:], pattern=[[FINE, X_COARSE]], base=-(NX // 2), channel_multiplier=0,
+            out=starts[:, 0:X_COARSE], pattern=[[FINE, X_COARSE]], base=-(NX // 2), channel_multiplier=0,
             allow_small_or_imprecise_dtypes=True,
         )
-        y_starts = keep.tile([P, Y_COARSE], F32)
         nc.gpsimd.iota(
-            out=y_starts[:], pattern=[[FINE, Y_COARSE]], base=0, channel_multiplier=0,
+            out=starts[:, X_COARSE:], pattern=[[FINE, Y_COARSE]], base=0, channel_multiplier=0,
             allow_small_or_imprecise_dtypes=True,
         )
         identity = keep.tile([P, P], F32)
@@ -167,17 +139,58 @@ def tile_adjoint_kernel(
         nc.vector.tensor_scalar(
             out=centring[:], in0=ky, scalar1=float(NY // 2), scalar2=None, op0=ALU.mult
         )
-
-        fine_x, half_cos_x, half_sin_x = angle_tables(
-            nc, tables, kx, steps[:], x_starts[:], X_COARSE, centring[:], "x"
+        fine_shape = [P, PLANES, FINE]
+        fine_angle_x = tables.tile(fine_shape, F32)
+        fine_angle_y = tables.tile(fine_shape, F32)
+        for fine_angle, rate in ((fine_angle_x, kx), (fine_angle_y, ky)):
+            nc.vector.tensor_tensor(
+                out=fine_angle[:],
+                in0=rate.unsqueeze(2).to_broadcast(fine_shape),
+                in1=steps[:].unsqueeze(1).to_broadcast(fine_shape),
+                op=ALU.mult,
+            )
+        coarse_shape = [P, PLANES, X_COARSE + Y_COARSE]
+        coarse_angle = tables.tile(coarse_shape, F32)
+        x_part, y_part = slice(0, X_COARSE), slice(X_COARSE, X_COARSE + Y_COARSE)
+        for part, n_coarse, rate in ((x_part, X_COARSE, kx), (y_part, Y_COARSE, ky)):
+            nc.vector.tensor_tensor(
+                out=coarse_angle[:, :, part],
+                in0=rate.unsqueeze(2).to_broadcast([P, PLANES, n_coarse]),
+                in1=starts[:, part].unsqueeze(1).to_broadcast([P, PLANES, n_coarse]),
+                op=ALU.mult,
+            )
+        nc.vector.tensor_tensor(
+            out=coarse_angle[:, :, x_part],
+            in0=coarse_angle[:, :, x_part],
+            in1=centring[:].unsqueeze(2).to_broadcast([P, PLANES, X_COARSE]),
+            op=ALU.subtract,
         )
+        fine_x, for_cos, for_sin, fine_y = wrap_all(
+            nc,
+            tables,
+            (
+                (fine_angle_x[:], fine_shape, 0.0, "fine_x"),
+                (coarse_angle[:], coarse_shape, 0.0, "cos"),
+                (coarse_angle[:], coarse_shape, -0.25, "sin"),
+                (fine_angle_y[:], fine_shape, 0.0, "fine_y"),
+            ),
+        )
+        half_cos = tables.tile(coarse_shape, F32)
+        nc.vector.tensor_scalar(out=half_cos[:], in0=for_cos[:], scalar1=0.5, scalar2=None, op0=ALU.mult)
+        half_sin = tables.tile(coarse_shape, F32)
+        nc.vector.tensor_scalar(
+            out=half_sin[:], in0=for_sin[:], scalar1=-0.5 * math.pi, scalar2=0.5, op0=ALU.add, op1=ALU.mult
+        )
+
         q_x = keep.tile([P, PLANES, 3 * NX], F32)
         for plane in range(PLANES):
             sines_x = stream.tile([P, 2, NX], F32)
-            half_angle_sines(nc, sines_x, fine_x, half_cos_x, half_sin_x, plane, X_COARSE)
+            half_angle_sines(
+                nc, sines_x, fine_x[:, plane, :], half_cos[:, plane, x_part], half_sin[:, plane, x_part], X_COARSE
+            )
             flat = sines_x[:].rearrange("p w x -> p (w x)")
             nc.vector.tensor_tensor(out=q_x[:, plane, 0 : 2 * NX], in0=flat, in1=flat, op=ALU.mult)
-            nc.vector.tensor_scalar(
+            nc.gpsimd.tensor_scalar(
                 out=q_x[:, plane, 2 * NX : 3 * NX], in0=q_x[:, plane, 0:NX],
                 scalar1=-1.0, scalar2=1.0, op0=ALU.mult, op1=ALU.add,
             )
@@ -199,7 +212,7 @@ def tile_adjoint_kernel(
                 a_planes = stream.tile([P, PACK, 2 * NX], BF16)
                 for t in range(PACK):
                     plane = g * PACK + t
-                    first_terms = stream.tile([P, 2 * NX], F32)
+                    first_terms = stream.tile([P, 2 * NX], F32, bufs=6)
                     nc.scalar.activation(
                         out=first_terms[:], in_=q_x[:, plane, 0 : 2 * NX], func=ACT.Identity,
                         bias=k_difference[:, c, plane : plane + 1],
@@ -210,8 +223,9 @@ def tile_adjoint_kernel(
                         scalar=k_im_plus2[:, c, plane : plane + 1], in1=first_terms[:],
                         op0=ALU.mult, op1=ALU.add,
                     )
-                a_grouped = stream.tile([P, 2 * NX, PACK], BF16, align_bytes=64)
-                nc.vector.tensor_copy(out=a_grouped[:], in_=a_planes[:].rearrange("p t w -> p w t"))
+                a_grouped = stream.tile([P, 2 * NX, PACK], BF16, tag="grouped", align_bytes=64)
+                to_view, from_view = side_by_side(a_grouped[:], a_planes[:])
+                nc.scalar.copy(out=to_view, in_=from_view)
                 quantise(
                     nc, a_grouped[:],
                     a_codes[:, g].rearrange("p w x -> p (w x)"),
@@ -225,29 +239,27 @@ def tile_adjoint_kernel(
         nc.vector.tensor_copy(out=density[:], in_=density_bf[:].rearrange("p o g t -> p (o g t)"))
         density_minus2 = keep.tile([P, PLANES], F32)
         nc.vector.tensor_scalar(out=density_minus2[:], in0=density[:], scalar1=-2.0, scalar2=None, op0=ALU.mult)
-        fine_y, half_cos_y, half_sin_y = angle_tables(
-            nc, tables, ky, steps[:], y_starts[:], Y_COARSE, None, "y"
-        )
         e_codes = keep.tile([P, PASSES, 3, NY], U32, align_bytes=64)
         e_scales = keep.tile([P, PASSES, 3, NY], U8, align_bytes=64)
         for g in range(PASSES):
             e_planes = stream.tile([P, PACK, 2, NY], BF16, bufs=2)
             for t in range(PACK):
                 plane = g * PACK + t
-                sines_y = stream.tile([P, 2, NY], F32)
-                half_angle_sines(nc, sines_y, fine_y, half_cos_y, half_sin_y, plane, Y_COARSE)
-                nc.scalar.activation(out=sines_y[:], in_=sines_y[:], func=ACT.Square)
+                sines_y = stream.tile([P, 2, NY], F32, bufs=2)
+                half_angle_sines(
+                    nc, sines_y, fine_y[:, plane, :], half_cos[:, plane, y_part], half_sin[:, plane, y_part], Y_COARSE
+                )
+                q_y = stream.tile([P, 2, NY], F32, bufs=2)
+                nc.vector.tensor_tensor(out=q_y[:], in0=sines_y[:], in1=sines_y[:], op=ALU.mult)
                 nc.scalar.activation(
-                    out=e_planes[:, t], in_=sines_y[:], func=ACT.Identity,
+                    out=e_planes[:, t], in_=q_y[:], func=ACT.Identity,
                     bias=density[:, plane : plane + 1], scale=density_minus2[:, plane : plane + 1],
                 )
             nc.vector.memset(e_planes[:, :, 1, 0:1], 0.0)
             for kind, which, sign in ((E_RE, 0, 1.0), (E_IM, 1, 1.0), (E_IM_NEG, 1, -1.0)):
-                e_grouped = stream.tile([P, NY, PACK], BF16, align_bytes=64)
-                nc.vector.tensor_scalar(
-                    out=e_grouped[:], in0=e_planes[:, :, which, :].rearrange("p t y -> p y t"),
-                    scalar1=sign, scalar2=None, op0=ALU.mult,
-                )
+                e_grouped = stream.tile([P, NY, PACK], BF16, tag="grouped", align_bytes=64)
+                to_view, from_view = side_by_side(e_grouped[:], e_planes[:, :, which, :])
+                nc.vector.tensor_scalar(out=to_view, in0=from_view, scalar1=sign, scalar2=None, op0=ALU.mult)
                 quantise(nc, e_grouped[:], e_codes[:, g, kind, :], e_scales[:, g, kind, :])
 
         combined_re = [sums.tile([P, NY], F32, name="combined_re_%d" % h) for h in range(X_TILES)]
@@ -281,11 +293,12 @@ def tile_adjoint_kernel(
                 nc.vector.tensor_tensor(out=im_s_re[:], in0=recon_im[:], in1=s_re, op=ALU.mult)
                 re_s_im = stream.tile([P, NY], F32)
                 nc.vector.tensor_tensor(out=re_s_im[:], in0=recon_re[:], in1=s_im, op=ALU.mult)
+                re_term = stream.tile([P, NY], F32)
+                nc.gpsimd.tensor_tensor(out=re_term[:], in0=re_s_re[:], in1=im_s_im[:], op=ALU.add)
                 im_term = stream.tile([P, NY], F32)
                 nc.gpsimd.tensor_tensor(out=im_term[:], in0=im_s_re[:], in1=re_s_im[:], op=ALU.subtract)
                 first_coil, last_coil = c == 0, c == COILS - 1
-                nc.tensor.matmul(out=combined_re[h][:], lhsT=identity[:], rhs=re_s_re[:], start=first_coil, stop=False)
-                nc.tensor.matmul(out=combined_re[h][:], lhsT=identity[:], rhs=im_s_im[:], start=False, stop=last_coil)
+                nc.tensor.matmul(out=combined_re[h][:], lhsT=identity[:], rhs=re_term[:], start=first_coil, stop=last_coil)
                 nc.tensor.matmul(out=combined_im[h][:], lhsT=identity[:], rhs=im_term[:], start=first_coil, stop=last_coil)
 
         out_rows = out.rearrange("b x y o -> (b x) (y o)")

@@ -190,7 +190,7 @@ def tile_adjoint_kernel(
             )
             flat = sines_x[:].rearrange("p w x -> p (w x)")
             nc.vector.tensor_tensor(out=q_x[:, plane, 0 : 2 * NX], in0=flat, in1=flat, op=ALU.mult)
-            nc.gpsimd.tensor_scalar(
+            nc.vector.tensor_scalar(
                 out=q_x[:, plane, 2 * NX : 3 * NX], in0=q_x[:, plane, 0:NX],
                 scalar1=-1.0, scalar2=1.0, op0=ALU.mult, op1=ALU.add,
             )
@@ -294,9 +294,9 @@ def tile_adjoint_kernel(
                 re_s_im = stream.tile([P, NY], F32)
                 nc.vector.tensor_tensor(out=re_s_im[:], in0=recon_re[:], in1=s_im, op=ALU.mult)
                 re_term = stream.tile([P, NY], F32)
-                nc.gpsimd.tensor_tensor(out=re_term[:], in0=re_s_re[:], in1=im_s_im[:], op=ALU.add)
+                nc.vector.tensor_tensor(out=re_term[:], in0=re_s_re[:], in1=im_s_im[:], op=ALU.add)
                 im_term = stream.tile([P, NY], F32)
-                nc.gpsimd.tensor_tensor(out=im_term[:], in0=im_s_re[:], in1=re_s_im[:], op=ALU.subtract)
+                nc.vector.tensor_tensor(out=im_term[:], in0=im_s_re[:], in1=re_s_im[:], op=ALU.subtract)
                 first_coil, last_coil = c == 0, c == COILS - 1
                 nc.tensor.matmul(out=combined_re[h][:], lhsT=identity[:], rhs=re_term[:], start=first_coil, stop=last_coil)
                 nc.tensor.matmul(out=combined_im[h][:], lhsT=identity[:], rhs=im_term[:], start=first_coil, stop=last_coil)

@@ -19,7 +19,9 @@ COILS, SAMPLES, NX, NY = 8, 1024, 256, 512
 PASSES = SAMPLES // K_PASS
 PLANES = PASSES * PACK
 X_TILES = NX // P
+assert X_TILES == PASSES
 FINE = 64
+AHEAD = 1
 RUN = 4
 X_COARSE = NX // FINE
 Y_COARSE = NY // FINE
@@ -205,35 +207,56 @@ def tile_adjoint_kernel(
         k_im_plus2 = keep.tile(k_shape, F32)
         nc.vector.tensor_scalar(out=k_im_plus2[:], in0=k_im_flat, scalar1=2.0, scalar2=None, op0=ALU.mult)
 
-        def quantised_a(c):
-            a_codes = coil_pool.tile([P, PASSES, 2, NX], U32, align_bytes=64)
-            a_scales = coil_pool.tile([P, PASSES, 2, NX], U8, align_bytes=64)
+        terms_of, planes_of, grouped_of, words_of = {}, {}, {}, {}
+
+        def start_a(c):
+            for plane in range(PLANES):
+                first_terms = stream.tile([P, 2 * NX], F32, bufs=PLANES)
+                nc.scalar.activation(
+                    out=first_terms[:], in_=q_x[:, plane, 0 : 2 * NX], func=ACT.Identity,
+                    bias=k_difference[:, c, plane : plane + 1],
+                    scale=k_re_minus2[:, c, plane : plane + 1],
+                )
+                terms_of[c, plane] = first_terms
+
+        def finish_a(c):
             for g in range(PASSES):
                 a_planes = stream.tile([P, PACK, 2 * NX], BF16)
                 for t in range(PACK):
                     plane = g * PACK + t
-                    first_terms = stream.tile([P, 2 * NX], F32, bufs=6)
-                    nc.scalar.activation(
-                        out=first_terms[:], in_=q_x[:, plane, 0 : 2 * NX], func=ACT.Identity,
-                        bias=k_difference[:, c, plane : plane + 1],
-                        scale=k_re_minus2[:, c, plane : plane + 1],
-                    )
                     nc.vector.scalar_tensor_tensor(
                         out=a_planes[:, t, :], in0=q_x[:, plane, NX : 3 * NX],
-                        scalar=k_im_plus2[:, c, plane : plane + 1], in1=first_terms[:],
+                        scalar=k_im_plus2[:, c, plane : plane + 1], in1=terms_of[c, plane][:],
                         op0=ALU.mult, op1=ALU.add,
                     )
-                a_grouped = stream.tile([P, 2 * NX, PACK], BF16, tag="grouped", align_bytes=64)
-                to_view, from_view = side_by_side(a_grouped[:], a_planes[:])
-                nc.scalar.copy(out=to_view, in_=from_view)
-                quantise(
-                    nc, a_grouped[:],
-                    a_codes[:, g].rearrange("p w x -> p (w x)"),
-                    a_scales[:, g].rearrange("p w x -> p (w x)"),
-                )
-            return a_codes, a_scales
+                planes_of[c, g] = a_planes
 
-        next_a = quantised_a(0)
+        def regroup_a(c, g):
+            a_grouped = stream.tile([P, 2 * NX, PACK], BF16, tag="grouped", align_bytes=64)
+            to_view, from_view = side_by_side(a_grouped[:], planes_of[c, g][:])
+            nc.scalar.copy(out=to_view, in_=from_view)
+            grouped_of[c, g] = a_grouped
+
+        def quantise_a(c, g):
+            if g == 0:
+                a_codes = coil_pool.tile([P, PASSES, 2, NX], U32, align_bytes=64)
+                a_scales = coil_pool.tile([P, PASSES, 2, NX], U8, align_bytes=64)
+                words_of[c] = (a_codes, a_scales)
+            a_codes, a_scales = words_of[c]
+            quantise(
+                nc, grouped_of[c, g][:],
+                a_codes[:, g].rearrange("p w x -> p (w x)"),
+                a_scales[:, g].rearrange("p w x -> p (w x)"),
+            )
+
+        def whole_a(c):
+            start_a(c)
+            finish_a(c)
+            for g in range(PASSES):
+                regroup_a(c, g)
+                quantise_a(c, g)
+
+        whole_a(0)
 
         density = keep.tile([P, PLANES], F32)
         nc.vector.tensor_copy(out=density[:], in_=density_bf[:].rearrange("p o g t -> p (o g t)"))
@@ -256,50 +279,75 @@ def tile_adjoint_kernel(
                     bias=density[:, plane : plane + 1], scale=density_minus2[:, plane : plane + 1],
                 )
             nc.vector.memset(e_planes[:, :, 1, 0:1], 0.0)
-            for kind, which, sign in ((E_RE, 0, 1.0), (E_IM, 1, 1.0), (E_IM_NEG, 1, -1.0)):
-                e_grouped = stream.tile([P, NY, PACK], BF16, tag="grouped", align_bytes=64)
-                to_view, from_view = side_by_side(e_grouped[:], e_planes[:, :, which, :])
-                nc.vector.tensor_scalar(out=to_view, in0=from_view, scalar1=sign, scalar2=None, op0=ALU.mult)
-                quantise(nc, e_grouped[:], e_codes[:, g, kind, :], e_scales[:, g, kind, :])
+            e_grouped = [
+                stream.tile([P, NY, PACK], BF16, name="e_grouped_%d" % kind, tag="grouped", align_bytes=64)
+                for kind in (E_RE, E_IM, E_IM_NEG)
+            ]
+            for kind in (E_RE, E_IM):
+                to_view, from_view = side_by_side(e_grouped[kind][:], e_planes[:, :, kind, :])
+                nc.vector.tensor_copy(out=to_view, in_=from_view)
+            nc.vector.tensor_scalar(
+                out=e_grouped[E_IM_NEG][:], in0=e_grouped[E_IM][:], scalar1=-1.0, scalar2=None, op0=ALU.mult
+            )
+            for kind in (E_RE, E_IM, E_IM_NEG):
+                quantise(nc, e_grouped[kind][:], e_codes[:, g, kind, :], e_scales[:, g, kind, :])
+        table_change = keep.tile([P, 1], F32)
+        nc.scalar.activation(out=table_change[:], in_=q_y[:, 0, 1:2], func=ACT.Sqrt)
 
         combined_re = [sums.tile([P, NY], F32, name="combined_re_%d" % h) for h in range(X_TILES)]
         combined_im = [sums.tile([P, NY], F32, name="combined_im_%d" % h) for h in range(X_TILES)]
-        for c in range(COILS):
-            a_codes, a_scales = next_a
-            if c + 1 < COILS:
-                next_a = quantised_a(c + 1)
-            for h in range(X_TILES):
-                x_cols = slice(h * P, (h + 1) * P)
-                recon_re = recon.tile([P, NY], F32)
-                recon_im = recon.tile([P, NY], F32)
-                for g in range(PASSES):
-                    for part, kind_for_re, kind_for_im in ((0, E_RE, E_IM), (1, E_IM_NEG, E_RE)):
-                        for acc, kind in ((recon_re, kind_for_re), (recon_im, kind_for_im)):
-                            nc.tensor.matmul_mx(
-                                out=acc[:],
-                                lhsT=a_codes[:, g, part, x_cols].bitcast(FP8X4),
-                                lhsT_scale=a_scales[:, g, part, x_cols],
-                                rhs=e_codes[:, g, kind, :].bitcast(FP8X4),
-                                rhs_scale=e_scales[:, g, kind, :],
-                                start=(g == 0 and part == 0),
-                                stop=(g == PASSES - 1 and part == 1),
-                            )
-                s_re, s_im = maps_re[:, c, h, :], maps_im[:, c, h, :]
-                re_s_re = stream.tile([P, NY], F32)
-                nc.vector.tensor_tensor(out=re_s_re[:], in0=recon_re[:], in1=s_re, op=ALU.mult)
-                im_s_im = stream.tile([P, NY], F32)
-                nc.vector.tensor_tensor(out=im_s_im[:], in0=recon_im[:], in1=s_im, op=ALU.mult)
-                im_s_re = stream.tile([P, NY], F32)
-                nc.vector.tensor_tensor(out=im_s_re[:], in0=recon_im[:], in1=s_re, op=ALU.mult)
-                re_s_im = stream.tile([P, NY], F32)
-                nc.vector.tensor_tensor(out=re_s_im[:], in0=recon_re[:], in1=s_im, op=ALU.mult)
-                re_term = stream.tile([P, NY], F32)
-                nc.vector.tensor_tensor(out=re_term[:], in0=re_s_re[:], in1=im_s_im[:], op=ALU.add)
-                im_term = stream.tile([P, NY], F32)
-                nc.vector.tensor_tensor(out=im_term[:], in0=im_s_re[:], in1=re_s_im[:], op=ALU.subtract)
-                first_coil, last_coil = c == 0, c == COILS - 1
-                nc.tensor.matmul(out=combined_re[h][:], lhsT=identity[:], rhs=re_term[:], start=first_coil, stop=last_coil)
-                nc.tensor.matmul(out=combined_im[h][:], lhsT=identity[:], rhs=im_term[:], start=first_coil, stop=last_coil)
+        def recon_matmuls(c, h):
+            a_codes, a_scales = words_of[c]
+            x_cols = slice(h * P, (h + 1) * P)
+            recon_re = recon.tile([P, NY], F32)
+            recon_im = recon.tile([P, NY], F32)
+            for g in range(PASSES):
+                for part, kind_for_re, kind_for_im in ((0, E_RE, E_IM), (1, E_IM_NEG, E_RE)):
+                    for acc, kind in ((recon_re, kind_for_re), (recon_im, kind_for_im)):
+                        nc.tensor.matmul_mx(
+                            out=acc[:],
+                            lhsT=a_codes[:, g, part, x_cols].bitcast(FP8X4),
+                            lhsT_scale=a_scales[:, g, part, x_cols],
+                            rhs=e_codes[:, g, kind, :].bitcast(FP8X4),
+                            rhs_scale=e_scales[:, g, kind, :],
+                            start=(g == 0 and part == 0),
+                            stop=(g == PASSES - 1 and part == 1),
+                        )
+            return recon_re, recon_im
+
+        def combine(c, h, recon_re, recon_im):
+            s_re, s_im = maps_re[:, c, h, :], maps_im[:, c, h, :]
+            re_s_re = stream.tile([P, NY], F32)
+            nc.vector.tensor_tensor(out=re_s_re[:], in0=recon_re[:], in1=s_re, op=ALU.mult)
+            im_s_im = stream.tile([P, NY], F32)
+            nc.vector.tensor_tensor(out=im_s_im[:], in0=recon_im[:], in1=s_im, op=ALU.mult)
+            im_s_re = stream.tile([P, NY], F32)
+            nc.vector.tensor_tensor(out=im_s_re[:], in0=recon_im[:], in1=s_re, op=ALU.mult)
+            re_s_im = stream.tile([P, NY], F32)
+            nc.vector.tensor_tensor(out=re_s_im[:], in0=recon_re[:], in1=s_im, op=ALU.mult)
+            first_coil, last_coil = c == 0, c == COILS - 1
+            nc.tensor.matmul(out=combined_re[h][:], lhsT=identity[:], rhs=re_s_re[:], start=first_coil, stop=False)
+            nc.tensor.matmul(out=combined_re[h][:], lhsT=identity[:], rhs=im_s_im[:], start=False, stop=last_coil)
+            im_term = stream.tile([P, NY], F32)
+            nc.vector.tensor_tensor(out=im_term[:], in0=im_s_re[:], in1=re_s_im[:], op=ALU.subtract)
+            nc.tensor.matmul(out=combined_im[h][:], lhsT=identity[:], rhs=im_term[:], start=first_coil, stop=last_coil)
+
+        for c in range(1, AHEAD):
+            whole_a(c)
+        with tc.manual_schedule():
+            for c in range(COILS):
+                making = c + AHEAD if c + AHEAD < COILS else None
+                if making is not None:
+                    start_a(making)
+                recons = [recon_matmuls(c, h) for h in range(X_TILES)]
+                if making is not None:
+                    finish_a(making)
+                    for g in range(PASSES):
+                        regroup_a(making, g)
+                for half in range(X_TILES):
+                    combine(c, half, recons[half][0], recons[half][1])
+                    if making is not None:
+                        quantise_a(making, half)
 
         out_rows = out.rearrange("b x y o -> (b x) (y o)")
         for h in range(X_TILES):

@@ -334,20 +334,19 @@ def tile_adjoint_kernel(
 
         for c in range(1, AHEAD):
             whole_a(c)
-        with tc.manual_schedule():
-            for c in range(COILS):
-                making = c + AHEAD if c + AHEAD < COILS else None
+        for c in range(COILS):
+            making = c + AHEAD if c + AHEAD < COILS else None
+            if making is not None:
+                start_a(making)
+            recons = [recon_matmuls(c, h) for h in range(X_TILES)]
+            if making is not None:
+                finish_a(making)
+                for g in range(PASSES):
+                    regroup_a(making, g)
+            for half in range(X_TILES):
+                combine(c, half, recons[half][0], recons[half][1])
                 if making is not None:
-                    start_a(making)
-                recons = [recon_matmuls(c, h) for h in range(X_TILES)]
-                if making is not None:
-                    finish_a(making)
-                    for g in range(PASSES):
-                        regroup_a(making, g)
-                for half in range(X_TILES):
-                    combine(c, half, recons[half][0], recons[half][1])
-                    if making is not None:
-                        quantise_a(making, half)
+                    quantise_a(making, half)
 
         out_rows = out.rearrange("b x y o -> (b x) (y o)")
         for h in range(X_TILES):

@@ -25,6 +25,7 @@ AHEAD = 1
 RUN = 4
 X_COARSE = NX // FINE
 Y_COARSE = NY // FINE
+Y_BLOCKS = NY // P
 
 TWO_PI = 2.0 * math.pi
 TWO_PI_HIGH = round(TWO_PI * 4096.0) / 4096.0
@@ -315,22 +316,31 @@ def tile_adjoint_kernel(
                         )
             return recon_re, recon_im
 
+        def add_transposed(total, term, first, last):
+            for j in range(Y_BLOCKS):
+                cols = slice(j * P, (j + 1) * P)
+                nc.tensor.matmul(
+                    out=total[:, cols], lhsT=term[:, cols], rhs=identity[:], is_transpose=True,
+                    start=(first and j == 0), stop=(last and j == Y_BLOCKS - 1),
+                )
+
         def combine(c, h, recon_re, recon_im):
             s_re, s_im = maps_re[:, c, h, :], maps_im[:, c, h, :]
+            first_coil, last_coil = c == 0, c == COILS - 1
             re_s_re = stream.tile([P, NY], F32)
             nc.vector.tensor_tensor(out=re_s_re[:], in0=recon_re[:], in1=s_re, op=ALU.mult)
+            add_transposed(combined_re[h], re_s_re, first_coil, False)
             im_s_im = stream.tile([P, NY], F32)
             nc.vector.tensor_tensor(out=im_s_im[:], in0=recon_im[:], in1=s_im, op=ALU.mult)
+            add_transposed(combined_re[h], im_s_im, False, last_coil)
             im_s_re = stream.tile([P, NY], F32)
             nc.vector.tensor_tensor(out=im_s_re[:], in0=recon_im[:], in1=s_re, op=ALU.mult)
+            add_transposed(combined_im[h], im_s_re, first_coil, False)
             re_s_im = stream.tile([P, NY], F32)
-            nc.vector.tensor_tensor(out=re_s_im[:], in0=recon_re[:], in1=s_im, op=ALU.mult)
-            first_coil, last_coil = c == 0, c == COILS - 1
-            nc.tensor.matmul(out=combined_re[h][:], lhsT=identity[:], rhs=re_s_re[:], start=first_coil, stop=False)
-            nc.tensor.matmul(out=combined_re[h][:], lhsT=identity[:], rhs=im_s_im[:], start=False, stop=last_coil)
-            im_term = stream.tile([P, NY], F32)
-            nc.vector.tensor_tensor(out=im_term[:], in0=im_s_re[:], in1=re_s_im[:], op=ALU.subtract)
-            nc.tensor.matmul(out=combined_im[h][:], lhsT=identity[:], rhs=im_term[:], start=first_coil, stop=last_coil)
+            nc.vector.scalar_tensor_tensor(
+                out=re_s_im[:], in0=recon_re[:], scalar=-1.0, in1=s_im, op0=ALU.mult, op1=ALU.mult
+            )
+            add_transposed(combined_im[h], re_s_im, False, last_coil)
 
         for c in range(1, AHEAD):
             whole_a(c)
@@ -354,8 +364,9 @@ def tile_adjoint_kernel(
             nc.scalar.activation(out=re_squared[:], in_=combined_re[h][:], func=ACT.Square)
             im_squared = ending.tile([P, NY], F32)
             nc.scalar.activation(out=im_squared[:], in_=combined_im[h][:], func=ACT.Square)
-            power = ending.tile([P, NY], F32)
-            nc.vector.tensor_tensor(out=power[:], in0=re_squared[:], in1=im_squared[:], op=ALU.add)
+            power = recon.tile([P, NY], F32, tag="recon_re")
+            add_transposed(power, re_squared, True, False)
+            add_transposed(power, im_squared, False, True)
             magnitude = ending.tile([P, NY], F32)
             nc.scalar.activation(out=magnitude[:], in_=power[:], func=ACT.Sqrt)
             nc.sync.dma_start(out=out_rows[h * P : (h + 1) * P, :], in_=magnitude[:])

@@ -22,6 +22,7 @@ X_TILES = NX // P
 assert X_TILES == PASSES
 FINE = 64
 AHEAD = 1
+TENSOR_COILS = 1
 RUN = 4
 X_COARSE = NX // FINE
 Y_COARSE = NY // FINE
@@ -135,6 +136,24 @@ def tile_adjoint_kernel(
         identity = keep.tile([P, P], F32)
         make_identity(nc, identity[:])
 
+        k_shape = [P, COILS, PLANES]
+        k_re_minus2 = keep.tile(k_shape, F32)
+        nc.vector.tensor_scalar(
+            out=k_re_minus2[:], in0=k_re_bf[:].rearrange("p c g t -> p c (g t)"), scalar1=-2.0, scalar2=None, op0=ALU.mult
+        )
+        k_im_plus2 = keep.tile(k_shape, F32)
+        nc.vector.tensor_scalar(
+            out=k_im_plus2[:], in0=k_im_bf[:].rearrange("p c g t -> p c (g t)"), scalar1=2.0, scalar2=None, op0=ALU.mult
+        )
+        diagonal = keep.tile([P, TENSOR_COILS, PLANES, 2, P], F32)
+        for c in range(TENSOR_COILS):
+            for plane in range(PLANES):
+                for term, factor in enumerate((k_re_minus2, k_im_plus2)):
+                    nc.scalar.activation(
+                        out=diagonal[:, c, plane, term, :], in_=identity[:], func=ACT.Copy,
+                        scale=factor[:, c, plane : plane + 1],
+                    )
+
         traj = keep.tile([P, 2, PLANES], F32)
         nc.vector.tensor_copy(out=traj[:], in_=traj_bf[:].rearrange("p a g t -> p a (g t)"))
         kx, ky = traj[:, 0, :], traj[:, 1, :]
@@ -192,21 +211,15 @@ def tile_adjoint_kernel(
                 nc, sines_x, fine_x[:, plane, :], half_cos[:, plane, x_part], half_sin[:, plane, x_part], X_COARSE
             )
             flat = sines_x[:].rearrange("p w x -> p (w x)")
-            nc.vector.tensor_tensor(out=q_x[:, plane, 0 : 2 * NX], in0=flat, in1=flat, op=ALU.mult)
+            squares_x = stream.tile([P, 2 * NX], F32)
+            nc.vector.tensor_tensor(out=squares_x[:], in0=flat, in1=flat, op=ALU.mult)
             nc.vector.tensor_scalar(
-                out=q_x[:, plane, 2 * NX : 3 * NX], in0=q_x[:, plane, 0:NX],
-                scalar1=-1.0, scalar2=1.0, op0=ALU.mult, op1=ALU.add,
+                out=q_x[:, plane, 0 : 2 * NX], in0=squares_x[:], scalar1=-0.5, scalar2=None, op0=ALU.add
             )
-
-        k_shape = [P, COILS, PLANES]
-        k_re_flat = k_re_bf[:].rearrange("p c g t -> p c (g t)")
-        k_im_flat = k_im_bf[:].rearrange("p c g t -> p c (g t)")
-        k_difference = keep.tile(k_shape, F32)
-        nc.vector.tensor_tensor(out=k_difference[:], in0=k_re_flat, in1=k_im_flat, op=ALU.subtract)
-        k_re_minus2 = keep.tile(k_shape, F32)
-        nc.vector.tensor_scalar(out=k_re_minus2[:], in0=k_re_flat, scalar1=-2.0, scalar2=None, op0=ALU.mult)
-        k_im_plus2 = keep.tile(k_shape, F32)
-        nc.vector.tensor_scalar(out=k_im_plus2[:], in0=k_im_flat, scalar1=2.0, scalar2=None, op0=ALU.mult)
+            nc.vector.tensor_scalar(
+                out=q_x[:, plane, 2 * NX : 3 * NX], in0=squares_x[:, 0:NX],
+                scalar1=-1.0, scalar2=0.5, op0=ALU.mult, op1=ALU.add,
+            )
 
         terms_of, planes_of, grouped_of, words_of = {}, {}, {}, {}
 
@@ -214,8 +227,7 @@ def tile_adjoint_kernel(
             for plane in range(PLANES):
                 first_terms = stream.tile([P, 2 * NX], F32, bufs=PLANES)
                 nc.scalar.activation(
-                    out=first_terms[:], in_=q_x[:, plane, 0 : 2 * NX], func=ACT.Identity,
-                    bias=k_difference[:, c, plane : plane + 1],
+                    out=first_terms[:], in_=q_x[:, plane, 0 : 2 * NX], func=ACT.Copy,
                     scale=k_re_minus2[:, c, plane : plane + 1],
                 )
                 terms_of[c, plane] = first_terms
@@ -257,7 +269,29 @@ def tile_adjoint_kernel(
                 regroup_a(c, g)
                 quantise_a(c, g)
 
-        whole_a(0)
+        def tensor_a(c, g, pool, tags):
+            a_sums = [pool.tile([P, PACK, P], F32, name="a_sum_%d" % j, tag=tags[j]) for j in range(len(tags))]
+            for t in range(PACK):
+                plane = g * PACK + t
+                for term in range(2):
+                    for j in range(len(tags)):
+                        nc.tensor.matmul(
+                            out=a_sums[j][:, t, :], lhsT=diagonal[:, c, plane, term, :],
+                            rhs=q_x[:, plane, term * NX + j * P : term * NX + (j + 1) * P],
+                            start=(t == 0 and term == 0), stop=(t == PACK - 1 and term == 1),
+                        )
+            a_grouped = stream.tile([P, 2 * NX, PACK], BF16, tag="grouped", align_bytes=64)
+            for j in range(len(tags)):
+                nc.scalar.copy(
+                    out=a_grouped[:, j * P : (j + 1) * P, :], in_=a_sums[j][:].rearrange("p t x -> p x t")
+                )
+            grouped_of[c, g] = a_grouped
+
+        for c in range(TENSOR_COILS):
+            tensor_a(c, 0, recon, ("recon_re", "recon_im", "recon_re", "recon_im"))
+            quantise_a(c, 0)
+            tensor_a(c, 1, sums, ("combined_re_0", "combined_re_1", "combined_im_0", "combined_im_1"))
+            quantise_a(c, 1)
 
         density = keep.tile([P, PLANES], F32)
         nc.vector.tensor_copy(out=density[:], in_=density_bf[:].rearrange("p o g t -> p (o g t)"))
@@ -274,10 +308,11 @@ def tile_adjoint_kernel(
                     nc, sines_y, fine_y[:, plane, :], half_cos[:, plane, y_part], half_sin[:, plane, y_part], Y_COARSE
                 )
                 q_y = stream.tile([P, 2, NY], F32, bufs=2)
-                nc.vector.tensor_tensor(out=q_y[:], in0=sines_y[:], in1=sines_y[:], op=ALU.mult)
-                nc.scalar.activation(
-                    out=e_planes[:, t], in_=q_y[:], func=ACT.Identity,
-                    bias=density[:, plane : plane + 1], scale=density_minus2[:, plane : plane + 1],
+                nc.scalar.activation(out=q_y[:], in_=sines_y[:], func=ACT.Square)
+                nc.vector.tensor_scalar(
+                    out=e_planes[:, t], in0=q_y[:],
+                    scalar1=density_minus2[:, plane : plane + 1], scalar2=density[:, plane : plane + 1],
+                    op0=ALU.mult, op1=ALU.add,
                 )
             nc.vector.memset(e_planes[:, :, 1, 0:1], 0.0)
             e_grouped = [
@@ -342,8 +377,6 @@ def tile_adjoint_kernel(
             )
             add_transposed(combined_im[h], re_s_im, False, last_coil)
 
-        for c in range(1, AHEAD):
-            whole_a(c)
         for c in range(COILS):
             making = c + AHEAD if c + AHEAD < COILS else None
             if making is not None:

@@ -136,6 +136,42 @@ def tile_adjoint_kernel(
         identity = keep.tile([P, P], F32)
         make_identity(nc, identity[:])
 
+        traj = keep.tile([P, 2, PLANES], F32)
+        nc.vector.tensor_copy(out=traj[:], in_=traj_bf[:].rearrange("p a g t -> p a (g t)"))
+        kx, ky = traj[:, 0, :], traj[:, 1, :]
+        centring = keep.tile([P, PLANES], F32)
+        nc.vector.tensor_scalar(
+            out=centring[:], in0=ky, scalar1=float(NY // 2), scalar2=None, op0=ALU.mult
+        )
+        fine_shape = [P, PLANES, FINE]
+        fine_angle_x = tables.tile(fine_shape, F32)
+        fine_angle_y = tables.tile(fine_shape, F32)
+
+        def fine_angles(fine_angle, rate):
+            nc.vector.tensor_tensor(
+                out=fine_angle[:],
+                in0=rate.unsqueeze(2).to_broadcast(fine_shape),
+                in1=steps[:].unsqueeze(1).to_broadcast(fine_shape),
+                op=ALU.mult,
+            )
+
+        fine_angles(fine_angle_x, kx)
+        coarse_shape = [P, PLANES, X_COARSE + Y_COARSE]
+        coarse_angle = tables.tile(coarse_shape, F32)
+        x_part, y_part = slice(0, X_COARSE), slice(X_COARSE, X_COARSE + Y_COARSE)
+        for part, n_coarse, rate in ((x_part, X_COARSE, kx), (y_part, Y_COARSE, ky)):
+            nc.vector.tensor_tensor(
+                out=coarse_angle[:, :, part],
+                in0=rate.unsqueeze(2).to_broadcast([P, PLANES, n_coarse]),
+                in1=starts[:, part].unsqueeze(1).to_broadcast([P, PLANES, n_coarse]),
+                op=ALU.mult,
+            )
+        nc.vector.tensor_tensor(
+            out=coarse_angle[:, :, x_part],
+            in0=coarse_angle[:, :, x_part],
+            in1=centring[:].unsqueeze(2).to_broadcast([P, PLANES, X_COARSE]),
+            op=ALU.subtract,
+        )
         k_shape = [P, COILS, PLANES]
         k_re_minus2 = keep.tile(k_shape, F32)
         nc.vector.tensor_scalar(
@@ -154,47 +190,13 @@ def tile_adjoint_kernel(
                         scale=factor[:, c, plane : plane + 1],
                     )
 
-        traj = keep.tile([P, 2, PLANES], F32)
-        nc.vector.tensor_copy(out=traj[:], in_=traj_bf[:].rearrange("p a g t -> p a (g t)"))
-        kx, ky = traj[:, 0, :], traj[:, 1, :]
-        centring = keep.tile([P, PLANES], F32)
-        nc.vector.tensor_scalar(
-            out=centring[:], in0=ky, scalar1=float(NY // 2), scalar2=None, op0=ALU.mult
-        )
-        fine_shape = [P, PLANES, FINE]
-        fine_angle_x = tables.tile(fine_shape, F32)
-        fine_angle_y = tables.tile(fine_shape, F32)
-        for fine_angle, rate in ((fine_angle_x, kx), (fine_angle_y, ky)):
-            nc.vector.tensor_tensor(
-                out=fine_angle[:],
-                in0=rate.unsqueeze(2).to_broadcast(fine_shape),
-                in1=steps[:].unsqueeze(1).to_broadcast(fine_shape),
-                op=ALU.mult,
-            )
-        coarse_shape = [P, PLANES, X_COARSE + Y_COARSE]
-        coarse_angle = tables.tile(coarse_shape, F32)
-        x_part, y_part = slice(0, X_COARSE), slice(X_COARSE, X_COARSE + Y_COARSE)
-        for part, n_coarse, rate in ((x_part, X_COARSE, kx), (y_part, Y_COARSE, ky)):
-            nc.vector.tensor_tensor(
-                out=coarse_angle[:, :, part],
-                in0=rate.unsqueeze(2).to_broadcast([P, PLANES, n_coarse]),
-                in1=starts[:, part].unsqueeze(1).to_broadcast([P, PLANES, n_coarse]),
-                op=ALU.mult,
-            )
-        nc.vector.tensor_tensor(
-            out=coarse_angle[:, :, x_part],
-            in0=coarse_angle[:, :, x_part],
-            in1=centring[:].unsqueeze(2).to_broadcast([P, PLANES, X_COARSE]),
-            op=ALU.subtract,
-        )
-        fine_x, for_cos, for_sin, fine_y = wrap_all(
+        fine_x, for_cos, for_sin = wrap_all(
             nc,
             tables,
             (
                 (fine_angle_x[:], fine_shape, 0.0, "fine_x"),
                 (coarse_angle[:], coarse_shape, 0.0, "cos"),
                 (coarse_angle[:], coarse_shape, -0.25, "sin"),
-                (fine_angle_y[:], fine_shape, 0.0, "fine_y"),
             ),
         )
         half_cos = tables.tile(coarse_shape, F32)
@@ -202,6 +204,13 @@ def tile_adjoint_kernel(
         half_sin = tables.tile(coarse_shape, F32)
         nc.vector.tensor_scalar(
             out=half_sin[:], in0=for_sin[:], scalar1=-0.5 * math.pi, scalar2=0.5, op0=ALU.add, op1=ALU.mult
+        )
+        fine_angles(fine_angle_y, ky)
+        half_shape = [P, PACK, FINE]
+        fine_y_of_pass = wrap_all(
+            nc,
+            tables,
+            [(fine_angle_y[:, g * PACK : (g + 1) * PACK, :], half_shape, 0.0, "fine_y_%d" % g) for g in range(PASSES)],
         )
 
         q_x = keep.tile([P, PLANES, 3 * NX], F32)
@@ -271,20 +280,24 @@ def tile_adjoint_kernel(
 
         def tensor_a(c, g, pool, tags):
             a_sums = [pool.tile([P, PACK, P], F32, name="a_sum_%d" % j, tag=tags[j]) for j in range(len(tags))]
-            for t in range(PACK):
+            banks = range(len(tags))
+            if g == 0:
+                order = [(t, j) for t in range(PACK) for j in banks]
+            else:
+                order = [(t, j) for j in banks for t in range(PACK)]
+            a_grouped = stream.tile([P, 2 * NX, PACK], BF16, tag="grouped", align_bytes=64)
+            for t, j in order:
                 plane = g * PACK + t
                 for term in range(2):
-                    for j in range(len(tags)):
-                        nc.tensor.matmul(
-                            out=a_sums[j][:, t, :], lhsT=diagonal[:, c, plane, term, :],
-                            rhs=q_x[:, plane, term * NX + j * P : term * NX + (j + 1) * P],
-                            start=(t == 0 and term == 0), stop=(t == PACK - 1 and term == 1),
-                        )
-            a_grouped = stream.tile([P, 2 * NX, PACK], BF16, tag="grouped", align_bytes=64)
-            for j in range(len(tags)):
-                nc.scalar.copy(
-                    out=a_grouped[:, j * P : (j + 1) * P, :], in_=a_sums[j][:].rearrange("p t x -> p x t")
-                )
+                    nc.tensor.matmul(
+                        out=a_sums[j][:, t, :], lhsT=diagonal[:, c, plane, term, :],
+                        rhs=q_x[:, plane, term * NX + j * P : term * NX + (j + 1) * P],
+                        start=(t == 0 and term == 0), stop=(t == PACK - 1 and term == 1),
+                    )
+                if t == PACK - 1:
+                    nc.vector.tensor_copy(
+                        out=a_grouped[:, j * P : (j + 1) * P, :], in_=a_sums[j][:].rearrange("p t x -> p x t")
+                    )
             grouped_of[c, g] = a_grouped
 
         for c in range(TENSOR_COILS):
@@ -305,7 +318,7 @@ def tile_adjoint_kernel(
                 plane = g * PACK + t
                 sines_y = stream.tile([P, 2, NY], F32, bufs=2)
                 half_angle_sines(
-                    nc, sines_y, fine_y[:, plane, :], half_cos[:, plane, y_part], half_sin[:, plane, y_part], Y_COARSE
+                    nc, sines_y, fine_y_of_pass[g][:, t, :], half_cos[:, plane, y_part], half_sin[:, plane, y_part], Y_COARSE
                 )
                 q_y = stream.tile([P, 2, NY], F32, bufs=2)
                 nc.scalar.activation(out=q_y[:], in_=sines_y[:], func=ACT.Square)

@@ -135,6 +135,8 @@ def tile_adjoint_kernel(
         )
         identity = keep.tile([P, P], F32)
         make_identity(nc, identity[:])
+        first_sine = keep.tile([P, 1], F32)
+        nc.scalar.activation(out=first_sine[:], in_=steps[:, 0:1], func=ACT.Sin)
 
         traj = keep.tile([P, 2, PLANES], F32)
         nc.vector.tensor_copy(out=traj[:], in_=traj_bf[:].rearrange("p a g t -> p a (g t)"))

@@ -408,13 +408,21 @@ def tile_adjoint_kernel(
 
         out_rows = out.rearrange("b x y o -> (b x) (y o)")
         for h in range(X_TILES):
-            re_squared = ending.tile([P, NY], F32)
-            nc.scalar.activation(out=re_squared[:], in_=combined_re[h][:], func=ACT.Square)
-            im_squared = ending.tile([P, NY], F32)
-            nc.scalar.activation(out=im_squared[:], in_=combined_im[h][:], func=ACT.Square)
-            power = recon.tile([P, NY], F32, tag="recon_re")
-            add_transposed(power, re_squared, True, False)
-            add_transposed(power, im_squared, False, True)
-            magnitude = ending.tile([P, NY], F32)
-            nc.scalar.activation(out=magnitude[:], in_=power[:], func=ACT.Sqrt)
-            nc.sync.dma_start(out=out_rows[h * P : (h + 1) * P, :], in_=magnitude[:])
+            for piece in range(2):
+                power = recon.tile([P, NY // 2], F32, tag=("recon_re", "recon_im")[piece])
+                cols = slice(piece * NY // 2, (piece + 1) * NY // 2)
+                blocks = range(piece * Y_BLOCKS // 2, (piece + 1) * Y_BLOCKS // 2)
+                squared = []
+                for name, total in (("re_squared", combined_re[h]), ("im_squared", combined_im[h])):
+                    square = ending.tile([P, NY // 2], F32, name=name, bufs=2)
+                    nc.scalar.activation(out=square[:], in_=total[:, cols], func=ACT.Square)
+                    squared.append(square)
+                for i, square in enumerate(squared):
+                    for n in range(len(blocks)):
+                        nc.tensor.matmul(
+                            out=power[:, n * P : (n + 1) * P], lhsT=square[:, n * P : (n + 1) * P], rhs=identity[:],
+                            is_transpose=True, start=(i == 0 and n == 0), stop=(i == 1 and n == len(blocks) - 1),
+                        )
+                magnitude = ending.tile([P, NY // 2], F32, bufs=2)
+                nc.scalar.activation(out=magnitude[:], in_=power[:], func=ACT.Sqrt)
+                nc.sync.dma_start(out=out_rows[h * P : (h + 1) * P, cols], in_=magnitude[:])

@@ -23,8 +23,12 @@ assert X_TILES == PASSES
 FINE = 64
 AHEAD = 1
 TENSOR_COILS = 1
+GROUP = 2
+GPSIMD_SAMPLE = 3
+GPSIMD_FROM = 2
 RUN = 4
-X_COARSE = NX // FINE
+HALF_X = NX // 2
+X_COARSE = HALF_X // FINE
 Y_COARSE = NY // FINE
 Y_BLOCKS = NY // P
 
@@ -34,6 +38,7 @@ TWO_PI_LOW = TWO_PI - TWO_PI_HIGH
 ROUNDER = 1.5 * 2.0**23
 
 E_RE, E_IM, E_IM_NEG = 0, 1, 2
+RE_HIGH, IM_HIGH, RE_LOW, IM_LOW = 0, 1, 2, 3
 
 FLOPS = 4 * 2 * COILS * NX * SAMPLES * NY
 
@@ -104,12 +109,12 @@ def tile_adjoint_kernel(
     ):
         traj_bf = keep.tile([P, 2, PASSES, PACK], BF16)
         nc.sync.dma_start(out=traj_bf[:], in_=by_plane(trajectory, "a"))
+        density_bf = keep.tile([P, 1, PASSES, PACK], BF16)
+        nc.sync.dma_start(out=density_bf[:], in_=by_plane(density_comp.rearrange("(o m) -> o m", o=1), "o"))
         k_re_bf = keep.tile([P, COILS, PASSES, PACK], BF16)
         nc.sync.dma_start(out=k_re_bf[:], in_=by_plane(kspace_real.rearrange("b c m -> (b c) m"), "c"))
         k_im_bf = keep.tile([P, COILS, PASSES, PACK], BF16)
         nc.sync.dma_start(out=k_im_bf[:], in_=by_plane(kspace_imag.rearrange("b c m -> (b c) m"), "c"))
-        density_bf = keep.tile([P, 1, PASSES, PACK], BF16)
-        nc.sync.dma_start(out=density_bf[:], in_=by_plane(density_comp.rearrange("(o m) -> o m", o=1), "o"))
 
         maps_re = keep.tile([P, COILS, X_TILES, NY], BF16)
         maps_im = keep.tile([P, COILS, X_TILES, NY], BF16)
@@ -126,7 +131,7 @@ def tile_adjoint_kernel(
         )
         starts = keep.tile([P, X_COARSE + Y_COARSE], F32)
         nc.gpsimd.iota(
-            out=starts[:, 0:X_COARSE], pattern=[[FINE, X_COARSE]], base=-(NX // 2), channel_multiplier=0,
+            out=starts[:, 0:X_COARSE], pattern=[[FINE, X_COARSE]], base=0, channel_multiplier=0,
             allow_small_or_imprecise_dtypes=True,
         )
         nc.gpsimd.iota(
@@ -141,10 +146,6 @@ def tile_adjoint_kernel(
         traj = keep.tile([P, 2, PLANES], F32)
         nc.vector.tensor_copy(out=traj[:], in_=traj_bf[:].rearrange("p a g t -> p a (g t)"))
         kx, ky = traj[:, 0, :], traj[:, 1, :]
-        centring = keep.tile([P, PLANES], F32)
-        nc.vector.tensor_scalar(
-            out=centring[:], in0=ky, scalar1=float(NY // 2), scalar2=None, op0=ALU.mult
-        )
         fine_shape = [P, PLANES, FINE]
         fine_angle_x = tables.tile(fine_shape, F32)
         fine_angle_y = tables.tile(fine_shape, F32)
@@ -161,37 +162,27 @@ def tile_adjoint_kernel(
         coarse_shape = [P, PLANES, X_COARSE + Y_COARSE]
         coarse_angle = tables.tile(coarse_shape, F32)
         x_part, y_part = slice(0, X_COARSE), slice(X_COARSE, X_COARSE + Y_COARSE)
-        for part, n_coarse, rate in ((x_part, X_COARSE, kx), (y_part, Y_COARSE, ky)):
-            nc.vector.tensor_tensor(
-                out=coarse_angle[:, :, part],
-                in0=rate.unsqueeze(2).to_broadcast([P, PLANES, n_coarse]),
-                in1=starts[:, part].unsqueeze(1).to_broadcast([P, PLANES, n_coarse]),
-                op=ALU.mult,
-            )
+        centre = X_COARSE + Y_COARSE // 2
+        half_kx = keep.tile([P, PLANES], F32)
+        nc.vector.tensor_scalar(out=half_kx[:], in0=kx, scalar1=0.5, scalar2=None, op0=ALU.mult)
+        nc.vector.tensor_tensor(
+            out=coarse_angle[:, :, x_part],
+            in0=kx.unsqueeze(2).to_broadcast([P, PLANES, X_COARSE]),
+            in1=starts[:, x_part].unsqueeze(1).to_broadcast([P, PLANES, X_COARSE]),
+            op=ALU.mult,
+        )
         nc.vector.tensor_tensor(
             out=coarse_angle[:, :, x_part],
             in0=coarse_angle[:, :, x_part],
-            in1=centring[:].unsqueeze(2).to_broadcast([P, PLANES, X_COARSE]),
-            op=ALU.subtract,
+            in1=half_kx[:].unsqueeze(2).to_broadcast([P, PLANES, X_COARSE]),
+            op=ALU.add,
         )
-        k_shape = [P, COILS, PLANES]
-        k_re_minus2 = keep.tile(k_shape, F32)
-        nc.vector.tensor_scalar(
-            out=k_re_minus2[:], in0=k_re_bf[:].rearrange("p c g t -> p c (g t)"), scalar1=-2.0, scalar2=None, op0=ALU.mult
+        nc.vector.tensor_tensor(
+            out=coarse_angle[:, :, y_part],
+            in0=ky.unsqueeze(2).to_broadcast([P, PLANES, Y_COARSE]),
+            in1=starts[:, y_part].unsqueeze(1).to_broadcast([P, PLANES, Y_COARSE]),
+            op=ALU.mult,
         )
-        k_im_plus2 = keep.tile(k_shape, F32)
-        nc.vector.tensor_scalar(
-            out=k_im_plus2[:], in0=k_im_bf[:].rearrange("p c g t -> p c (g t)"), scalar1=2.0, scalar2=None, op0=ALU.mult
-        )
-        diagonal = keep.tile([P, TENSOR_COILS, PLANES, 2, P], F32)
-        for c in range(TENSOR_COILS):
-            for plane in range(PLANES):
-                for term, factor in enumerate((k_re_minus2, k_im_plus2)):
-                    nc.scalar.activation(
-                        out=diagonal[:, c, plane, term, :], in_=identity[:], func=ACT.Copy,
-                        scale=factor[:, c, plane : plane + 1],
-                    )
-
         fine_x, for_cos, for_sin = wrap_all(
             nc,
             tables,
@@ -207,6 +198,44 @@ def tile_adjoint_kernel(
         nc.vector.tensor_scalar(
             out=half_sin[:], in0=for_sin[:], scalar1=-0.5 * math.pi, scalar2=0.5, op0=ALU.add, op1=ALU.mult
         )
+        centre_sines = keep.tile([P, 2, PLANES], F32)
+        for which, half in enumerate((half_cos, half_sin)):
+            nc.vector.scalar_tensor_tensor(
+                out=centre_sines[:, which, :], in0=half_kx[:], scalar=0.5, in1=half[:, :, centre],
+                op0=ALU.mult, op1=ALU.add,
+            )
+        centre_squares = keep.tile([P, 2, PLANES], F32)
+        nc.scalar.activation(out=centre_sines[:], in_=centre_sines[:], func=ACT.Sin)
+        nc.scalar.activation(out=centre_squares[:], in_=centre_sines[:], func=ACT.Square)
+        centre_factors = keep.tile([P, 2, PLANES], F32)
+        nc.vector.tensor_scalar(
+            out=centre_factors[:], in0=centre_squares[:], scalar1=-4.0, scalar2=2.0, op0=ALU.mult, op1=ALU.add
+        )
+        k_shape = [P, COILS, PLANES]
+        k_re = k_re_bf[:].rearrange("p c g t -> p c (g t)")
+        k_im = k_im_bf[:].rearrange("p c g t -> p c (g t)")
+        two_cos, two_sin = (centre_factors[:, i, :].unsqueeze(1).to_broadcast(k_shape) for i in range(2))
+        kappa_re = keep.tile(k_shape, F32)
+        kappa_im = keep.tile(k_shape, F32)
+        re_by_cos = keep.tile(k_shape, F32)
+        im_by_sin = keep.tile(k_shape, F32)
+        im_by_cos = keep.tile(k_shape, F32)
+        re_by_sin = keep.tile(k_shape, F32)
+        nc.vector.tensor_tensor(out=re_by_cos[:], in0=k_re, in1=two_cos, op=ALU.mult)
+        nc.vector.tensor_tensor(out=im_by_sin[:], in0=k_im, in1=two_sin, op=ALU.mult)
+        nc.vector.tensor_tensor(out=im_by_cos[:], in0=k_im, in1=two_cos, op=ALU.mult)
+        nc.vector.tensor_tensor(out=re_by_sin[:], in0=k_re, in1=two_sin, op=ALU.mult)
+        nc.vector.tensor_tensor(out=kappa_re[:], in0=re_by_cos[:], in1=im_by_sin[:], op=ALU.add)
+        nc.vector.tensor_tensor(out=kappa_im[:], in0=im_by_cos[:], in1=re_by_sin[:], op=ALU.subtract)
+        diagonal = keep.tile([P, TENSOR_COILS, PLANES, 2, P], F32)
+        for c in range(TENSOR_COILS):
+            for plane in range(PLANES):
+                for term, factor in enumerate((kappa_re, kappa_im)):
+                    nc.scalar.activation(
+                        out=diagonal[:, c, plane, term, :], in_=identity[:], func=ACT.Copy,
+                        scale=factor[:, c, plane : plane + 1],
+                    )
+
         fine_angles(fine_angle_y, ky)
         half_shape = [P, PACK, FINE]
         fine_y_of_pass = wrap_all(
@@ -215,56 +244,101 @@ def tile_adjoint_kernel(
             [(fine_angle_y[:, g * PACK : (g + 1) * PACK, :], half_shape, 0.0, "fine_y_%d" % g) for g in range(PASSES)],
         )
 
-        q_x = keep.tile([P, PLANES, 3 * NX], F32)
-        for plane in range(PLANES):
-            sines_x = stream.tile([P, 2, NX], F32)
-            half_angle_sines(
-                nc, sines_x, fine_x[:, plane, :], half_cos[:, plane, x_part], half_sin[:, plane, x_part], X_COARSE
-            )
-            flat = sines_x[:].rearrange("p w x -> p (w x)")
-            squares_x = stream.tile([P, 2 * NX], F32)
-            nc.vector.tensor_tensor(out=squares_x[:], in0=flat, in1=flat, op=ALU.mult)
+        q_x = keep.tile([P, PLANES, 4 * HALF_X], F32)
+        for first in range(0, PLANES, GROUP):
+            planes = slice(first, first + GROUP)
+            sines_x = stream.tile([P, GROUP, 2 * HALF_X], F32)
+            for i in range(GROUP):
+                half_angle_sines(
+                    nc, sines_x[:, i].rearrange("p (w x) -> p w x", w=2), fine_x[:, first + i, :],
+                    half_cos[:, first + i, x_part], half_sin[:, first + i, x_part], X_COARSE,
+                )
+            squares_x = stream.tile([P, GROUP, 2 * HALF_X], F32)
+            nc.vector.tensor_tensor(out=squares_x[:], in0=sines_x[:], in1=sines_x[:], op=ALU.mult)
             nc.vector.tensor_scalar(
-                out=q_x[:, plane, 0 : 2 * NX], in0=squares_x[:], scalar1=-0.5, scalar2=None, op0=ALU.add
+                out=q_x[:, planes, HALF_X : 3 * HALF_X], in0=squares_x[:], scalar1=-1.0, scalar2=0.5,
+                op0=ALU.mult, op1=ALU.add,
             )
             nc.vector.tensor_scalar(
-                out=q_x[:, plane, 2 * NX : 3 * NX], in0=squares_x[:, 0:NX],
-                scalar1=-1.0, scalar2=0.5, op0=ALU.mult, op1=ALU.add,
+                out=q_x[:, planes, 0:HALF_X], in0=squares_x[:, :, HALF_X:], scalar1=-0.5, scalar2=None, op0=ALU.add
+            )
+            nc.vector.tensor_scalar(
+                out=q_x[:, planes, 3 * HALF_X :], in0=squares_x[:, :, 0:HALF_X], scalar1=-0.5, scalar2=None, op0=ALU.add
             )
 
         terms_of, planes_of, grouped_of, words_of = {}, {}, {}, {}
 
-        def start_a(c):
-            for plane in range(PLANES):
-                first_terms = stream.tile([P, 2 * NX], F32, bufs=PLANES)
+        def start_planes(c):
+            planes_of[c] = stream.tile([P, PASSES, PACK, 2 * NX], BF16, name="a_planes")
+
+        def gpsimd_a(c):
+            start_planes(c)
+            firsts = stream.tile([P, PASSES, NX], F32, bufs=1)
+            seconds = stream.tile([P, PASSES, NX], F32, tag="last_terms", bufs=1)
+            for g in range(PASSES):
+                plane = g * PACK + GPSIMD_SAMPLE
                 nc.scalar.activation(
-                    out=first_terms[:], in_=q_x[:, plane, 0 : 2 * NX], func=ACT.Copy,
-                    scale=k_re_minus2[:, c, plane : plane + 1],
+                    out=firsts[:, g, :], in_=q_x[:, plane, HALF_X : 3 * HALF_X], func=ACT.Copy,
+                    scale=kappa_re[:, c, plane : plane + 1],
+                )
+            for g in range(PASSES):
+                plane = g * PACK + GPSIMD_SAMPLE
+                nc.scalar.activation(
+                    out=seconds[:, g, :], in_=q_x[:, plane, 0 : 2 * HALF_X], func=ACT.Copy,
+                    scale=kappa_im[:, c, plane : plane + 1],
+                )
+            for op, cols in ((ALU.add, slice(0, NX)), (ALU.subtract, slice(NX, 2 * NX))):
+                nc.gpsimd.tensor_tensor(
+                    out=planes_of[c][:, :, GPSIMD_SAMPLE, cols], in0=firsts[:], in1=seconds[:], op=op
+                )
+
+        def vector_planes(c):
+            return [p for p in range(PLANES) if c < GPSIMD_FROM or p % PACK != GPSIMD_SAMPLE]
+
+        def start_a(c):
+            planes = vector_planes(c)
+            for plane in planes:
+                if plane == planes[-1]:
+                    first_terms = stream.tile([P, NX], F32, name="last_terms", tag="last_terms", bufs=1)
+                else:
+                    first_terms = stream.tile([P, NX], F32, bufs=PLANES - 1)
+                nc.scalar.activation(
+                    out=first_terms[:], in_=q_x[:, plane, HALF_X : 3 * HALF_X], func=ACT.Copy,
+                    scale=kappa_re[:, c, plane : plane + 1],
                 )
                 terms_of[c, plane] = first_terms
 
         def finish_a(c):
-            for g in range(PASSES):
-                a_planes = stream.tile([P, PACK, 2 * NX], BF16)
-                for t in range(PACK):
-                    plane = g * PACK + t
-                    nc.vector.scalar_tensor_tensor(
-                        out=a_planes[:, t, :], in0=q_x[:, plane, NX : 3 * NX],
-                        scalar=k_im_plus2[:, c, plane : plane + 1], in1=terms_of[c, plane][:],
-                        op0=ALU.mult, op1=ALU.add,
-                    )
-                planes_of[c, g] = a_planes
+            if c < GPSIMD_FROM:
+                start_planes(c)
+            for plane in vector_planes(c):
+                g, t = divmod(plane, PACK)
+                nc.vector.scalar_tensor_tensor(
+                    out=planes_of[c][:, g, t, :].rearrange("p (s x) -> p s x", s=2),
+                    in0=q_x[:, plane, :].rearrange("p (s x) -> p s x", s=2),
+                    scalar=kappa_im[:, c, plane : plane + 1],
+                    in1=terms_of[c, plane][:].unsqueeze(1).to_broadcast([P, 2, NX]),
+                    op0=ALU.mult, op1=ALU.add,
+                )
 
         def regroup_a(c, g):
             a_grouped = stream.tile([P, 2 * NX, PACK], BF16, tag="grouped", align_bytes=64)
-            to_view, from_view = side_by_side(a_grouped[:], planes_of[c, g][:])
+            a_planes = planes_of[c][:, g]
+            to_view, from_view = side_by_side(a_grouped[:, 0:NX], a_planes[:, :, 0:NX])
             nc.scalar.copy(out=to_view, in_=from_view)
+            for block in (RE_LOW, IM_LOW):
+                cols = slice(block * HALF_X, (block + 1) * HALF_X)
+                to_view, from_view = side_by_side(a_grouped[:, cols], a_planes[:, :, cols][:, :, ::-1])
+                if block == RE_LOW:
+                    nc.scalar.copy(out=to_view, in_=from_view)
+                else:
+                    nc.scalar.activation(out=to_view, in_=from_view, func=ACT.Copy, scale=-1.0)
             grouped_of[c, g] = a_grouped
 
         def quantise_a(c, g):
             if g == 0:
-                a_codes = coil_pool.tile([P, PASSES, 2, NX], U32, align_bytes=64)
-                a_scales = coil_pool.tile([P, PASSES, 2, NX], U8, align_bytes=64)
+                a_codes = coil_pool.tile([P, PASSES, 4, HALF_X], U32, align_bytes=64)
+                a_scales = coil_pool.tile([P, PASSES, 4, HALF_X], U8, align_bytes=64)
                 words_of[c] = (a_codes, a_scales)
             a_codes, a_scales = words_of[c]
             quantise(
@@ -290,16 +364,21 @@ def tile_adjoint_kernel(
             a_grouped = stream.tile([P, 2 * NX, PACK], BF16, tag="grouped", align_bytes=64)
             for t, j in order:
                 plane = g * PACK + t
-                for term in range(2):
+                for term, block in enumerate((1 + j % 2, j)):
                     nc.tensor.matmul(
                         out=a_sums[j][:, t, :], lhsT=diagonal[:, c, plane, term, :],
-                        rhs=q_x[:, plane, term * NX + j * P : term * NX + (j + 1) * P],
+                        rhs=q_x[:, plane, block * HALF_X : (block + 1) * HALF_X],
                         start=(t == 0 and term == 0), stop=(t == PACK - 1 and term == 1),
                     )
                 if t == PACK - 1:
-                    nc.vector.tensor_copy(
-                        out=a_grouped[:, j * P : (j + 1) * P, :], in_=a_sums[j][:].rearrange("p t x -> p x t")
-                    )
+                    to_view = a_grouped[:, j * P : (j + 1) * P, :]
+                    from_view = a_sums[j][:].rearrange("p t x -> p x t")
+                    if j in (RE_LOW, IM_LOW):
+                        from_view = from_view[:, ::-1, :]
+                    if j == IM_LOW:
+                        nc.vector.tensor_scalar(out=to_view, in0=from_view, scalar1=-1.0, scalar2=None, op0=ALU.mult)
+                    else:
+                        nc.vector.tensor_copy(out=to_view, in_=from_view)
             grouped_of[c, g] = a_grouped
 
         for c in range(TENSOR_COILS):
@@ -349,20 +428,20 @@ def tile_adjoint_kernel(
         combined_im = [sums.tile([P, NY], F32, name="combined_im_%d" % h) for h in range(X_TILES)]
         def recon_matmuls(c, h):
             a_codes, a_scales = words_of[c]
-            x_cols = slice(h * P, (h + 1) * P)
+            a_re, a_im = (RE_LOW, IM_LOW) if h == 0 else (RE_HIGH, IM_HIGH)
             recon_re = recon.tile([P, NY], F32)
             recon_im = recon.tile([P, NY], F32)
             for g in range(PASSES):
-                for part, kind_for_re, kind_for_im in ((0, E_RE, E_IM), (1, E_IM_NEG, E_RE)):
+                for block, kind_for_re, kind_for_im in ((a_re, E_RE, E_IM), (a_im, E_IM_NEG, E_RE)):
                     for acc, kind in ((recon_re, kind_for_re), (recon_im, kind_for_im)):
                         nc.tensor.matmul_mx(
                             out=acc[:],
-                            lhsT=a_codes[:, g, part, x_cols].bitcast(FP8X4),
-                            lhsT_scale=a_scales[:, g, part, x_cols],
+                            lhsT=a_codes[:, g, block, :].bitcast(FP8X4),
+                            lhsT_scale=a_scales[:, g, block, :],
                             rhs=e_codes[:, g, kind, :].bitcast(FP8X4),
                             rhs_scale=e_scales[:, g, kind, :],
-                            start=(g == 0 and part == 0),
-                            stop=(g == PASSES - 1 and part == 1),
+                            start=(g == 0 and block == a_re),
+                            stop=(g == PASSES - 1 and block == a_im),
                         )
             return recon_re, recon_im
 
@@ -399,12 +478,15 @@ def tile_adjoint_kernel(
             recons = [recon_matmuls(c, h) for h in range(X_TILES)]
             if making is not None:
                 finish_a(making)
+                if making + 1 < COILS:
+                    gpsimd_a(making + 1)
                 for g in range(PASSES):
                     regroup_a(making, g)
             for half in range(X_TILES):
                 combine(c, half, recons[half][0], recons[half][1])
-                if making is not None:
-                    quantise_a(making, half)
+            if making is not None:
+                for g in range(PASSES):
+                    quantise_a(making, g)
 
         out_rows = out.rearrange("b x y o -> (b x) (y o)")
         for h in range(X_TILES):

@@ -29,7 +29,12 @@ GPSIMD_FROM = 2
 RUN = 4
 HALF_X = NX // 2
 X_COARSE = HALF_X // FINE
-Y_COARSE = NY // FINE
+Y_SPAN = 2 * FINE
+Y_COARSE = NY // Y_SPAN
+X_PART, Y_PART = slice(0, X_COARSE), slice(X_COARSE, X_COARSE + Y_COARSE)
+CENTRE = X_COARSE + Y_COARSE
+N_COARSE = CENTRE + 1
+OUTER = slice(X_COARSE, N_COARSE)
 Y_BLOCKS = NY // P
 
 TWO_PI = 2.0 * math.pi
@@ -48,17 +53,19 @@ def by_plane(vector_ap, lead):
 
 
 def wrap_all(nc, pool, jobs):
-    turns = [pool.tile(shape, F32, name="turns_" + label) for angle, shape, turn_shift, label in jobs]
-    wrapped = [pool.tile(shape, F32, name="wrapped_" + label) for angle, shape, turn_shift, label in jobs]
-    for i, (angle, shape, turn_shift, label) in enumerate(jobs):
+    turns = [pool.tile(shape, F32, name="turns_" + label) for angle, given, shape, turn_shift, label in jobs]
+    wrapped = [pool.tile(shape, F32, name="wrapped_" + label) for angle, given, shape, turn_shift, label in jobs]
+    for i, (angle, given, shape, turn_shift, label) in enumerate(jobs):
+        if given is None:
+            nc.vector.tensor_scalar(
+                out=turns[i][:], in0=angle, scalar1=1.0 / TWO_PI, scalar2=turn_shift, op0=ALU.mult, op1=ALU.add
+            )
+    for i, (angle, given, shape, turn_shift, label) in enumerate(jobs):
         nc.vector.tensor_scalar(
-            out=turns[i][:], in0=angle, scalar1=1.0 / TWO_PI, scalar2=turn_shift, op0=ALU.mult, op1=ALU.add
+            out=turns[i][:], in0=turns[i][:] if given is None else given[:],
+            scalar1=ROUNDER, scalar2=ROUNDER, op0=ALU.add, op1=ALU.subtract,
         )
-    for i in range(len(jobs)):
-        nc.vector.tensor_scalar(
-            out=turns[i][:], in0=turns[i][:], scalar1=ROUNDER, scalar2=ROUNDER, op0=ALU.add, op1=ALU.subtract
-        )
-    for i, (angle, shape, turn_shift, label) in enumerate(jobs):
+    for i, (angle, given, shape, turn_shift, label) in enumerate(jobs):
         nc.vector.scalar_tensor_tensor(
             out=wrapped[i][:], in0=turns[i][:], scalar=-TWO_PI_HIGH, in1=angle, op0=ALU.mult, op1=ALU.add
         )
@@ -102,7 +109,7 @@ def tile_adjoint_kernel(
         tc.tile_pool(name="keep", bufs=1) as keep,
         tc.tile_pool(name="tables", bufs=1) as tables,
         tc.tile_pool(name="stream", bufs=3) as stream,
-        tc.tile_pool(name="coil", bufs=4) as coil_pool,
+        tc.tile_pool(name="coil", bufs=3) as coil_pool,
         tc.tile_pool(name="ending", bufs=1) as ending,
         tc.psum_pool(name="sums", bufs=1) as sums,
         tc.psum_pool(name="recon", bufs=2) as recon,
@@ -129,13 +136,21 @@ def tile_adjoint_kernel(
             out=steps[:], pattern=[[1, FINE]], base=0, channel_multiplier=0,
             allow_small_or_imprecise_dtypes=True,
         )
-        starts = keep.tile([P, X_COARSE + Y_COARSE], F32)
+        nc.gpsimd.tensor_scalar(out=steps[:], in0=steps[:], scalar1=0.5, scalar2=None, op0=ALU.add)
+        starts = keep.tile([P, N_COARSE], F32)
         nc.gpsimd.iota(
-            out=starts[:, 0:X_COARSE], pattern=[[FINE, X_COARSE]], base=0, channel_multiplier=0,
+            out=starts[:, X_PART], pattern=[[FINE, X_COARSE]], base=0, channel_multiplier=0,
             allow_small_or_imprecise_dtypes=True,
         )
         nc.gpsimd.iota(
-            out=starts[:, X_COARSE:], pattern=[[FINE, Y_COARSE]], base=0, channel_multiplier=0,
+            out=starts[:, Y_PART], pattern=[[Y_SPAN, Y_COARSE]], base=FINE, channel_multiplier=0,
+            allow_small_or_imprecise_dtypes=True,
+        )
+        nc.gpsimd.tensor_scalar(
+            out=starts[:, Y_PART], in0=starts[:, Y_PART], scalar1=-0.5, scalar2=None, op0=ALU.add
+        )
+        nc.gpsimd.iota(
+            out=starts[:, CENTRE : CENTRE + 1], pattern=[[1, 1]], base=NY // 2, channel_multiplier=0,
             allow_small_or_imprecise_dtypes=True,
         )
         identity = keep.tile([P, P], F32)
@@ -150,71 +165,57 @@ def tile_adjoint_kernel(
         fine_angle_x = tables.tile(fine_shape, F32)
         fine_angle_y = tables.tile(fine_shape, F32)
 
-        def fine_angles(fine_angle, rate):
+        fine_turns_x = tables.tile(fine_shape, F32)
+        fine_turns_y = tables.tile(fine_shape, F32)
+        for fine_angle, fine_turns, rate in ((fine_angle_x, fine_turns_x, kx), (fine_angle_y, fine_turns_y, ky)):
+            for plane in range(PLANES):
+                nc.scalar.activation(
+                    out=fine_angle[:, plane, :], in_=steps[:], func=ACT.Copy, scale=rate[:, plane : plane + 1]
+                )
+            nc.scalar.activation(out=fine_turns[:], in_=fine_angle[:], func=ACT.Copy, scale=1.0 / TWO_PI)
+
+        coarse_shape = [P, PLANES, N_COARSE]
+        coarse_angle = tables.tile(coarse_shape, F32)
+        for part, rate in ((X_PART, kx), (OUTER, ky)):
+            shape = [P, PLANES, part.stop - part.start]
             nc.vector.tensor_tensor(
-                out=fine_angle[:],
-                in0=rate.unsqueeze(2).to_broadcast(fine_shape),
-                in1=steps[:].unsqueeze(1).to_broadcast(fine_shape),
+                out=coarse_angle[:, :, part],
+                in0=rate.unsqueeze(2).to_broadcast(shape),
+                in1=starts[:, part].unsqueeze(1).to_broadcast(shape),
                 op=ALU.mult,
             )
-
-        fine_angles(fine_angle_x, kx)
-        coarse_shape = [P, PLANES, X_COARSE + Y_COARSE]
-        coarse_angle = tables.tile(coarse_shape, F32)
-        x_part, y_part = slice(0, X_COARSE), slice(X_COARSE, X_COARSE + Y_COARSE)
-        centre = X_COARSE + Y_COARSE // 2
-        half_kx = keep.tile([P, PLANES], F32)
-        nc.vector.tensor_scalar(out=half_kx[:], in0=kx, scalar1=0.5, scalar2=None, op0=ALU.mult)
-        nc.vector.tensor_tensor(
-            out=coarse_angle[:, :, x_part],
-            in0=kx.unsqueeze(2).to_broadcast([P, PLANES, X_COARSE]),
-            in1=starts[:, x_part].unsqueeze(1).to_broadcast([P, PLANES, X_COARSE]),
-            op=ALU.mult,
-        )
-        nc.vector.tensor_tensor(
-            out=coarse_angle[:, :, x_part],
-            in0=coarse_angle[:, :, x_part],
-            in1=half_kx[:].unsqueeze(2).to_broadcast([P, PLANES, X_COARSE]),
-            op=ALU.add,
-        )
-        nc.vector.tensor_tensor(
-            out=coarse_angle[:, :, y_part],
-            in0=ky.unsqueeze(2).to_broadcast([P, PLANES, Y_COARSE]),
-            in1=starts[:, y_part].unsqueeze(1).to_broadcast([P, PLANES, Y_COARSE]),
-            op=ALU.mult,
-        )
         fine_x, for_cos, for_sin = wrap_all(
             nc,
             tables,
             (
-                (fine_angle_x[:], fine_shape, 0.0, "fine_x"),
-                (coarse_angle[:], coarse_shape, 0.0, "cos"),
-                (coarse_angle[:], coarse_shape, -0.25, "sin"),
+                (fine_angle_x[:], fine_turns_x, fine_shape, 0.0, "fine_x"),
+                (coarse_angle[:], None, coarse_shape, 0.0, "cos"),
+                (coarse_angle[:], None, coarse_shape, -0.25, "sin"),
             ),
         )
-        half_cos = tables.tile(coarse_shape, F32)
-        nc.vector.tensor_scalar(out=half_cos[:], in0=for_cos[:], scalar1=0.5, scalar2=None, op0=ALU.mult)
-        half_sin = tables.tile(coarse_shape, F32)
+        halves = tables.tile([P, 2] + coarse_shape[1:], F32)
+        half_cos, half_sin = halves[:, 0], halves[:, 1]
+        nc.vector.tensor_scalar(out=half_cos, in0=for_cos[:], scalar1=0.5, scalar2=None, op0=ALU.mult)
         nc.vector.tensor_scalar(
-            out=half_sin[:], in0=for_sin[:], scalar1=-0.5 * math.pi, scalar2=0.5, op0=ALU.add, op1=ALU.mult
+            out=half_sin, in0=for_sin[:], scalar1=-0.5 * math.pi, scalar2=0.5, op0=ALU.add, op1=ALU.mult
         )
-        centre_sines = keep.tile([P, 2, PLANES], F32)
-        for which, half in enumerate((half_cos, half_sin)):
-            nc.vector.scalar_tensor_tensor(
-                out=centre_sines[:, which, :], in0=half_kx[:], scalar=0.5, in1=half[:, :, centre],
-                op0=ALU.mult, op1=ALU.add,
-            )
-        centre_squares = keep.tile([P, 2, PLANES], F32)
-        nc.scalar.activation(out=centre_sines[:], in_=centre_sines[:], func=ACT.Sin)
-        nc.scalar.activation(out=centre_squares[:], in_=centre_sines[:], func=ACT.Square)
-        centre_factors = keep.tile([P, 2, PLANES], F32)
+        nc.vector.scalar_tensor_tensor(
+            out=halves[:, :, :, CENTRE], in0=kx.unsqueeze(1).to_broadcast([P, 2, PLANES]), scalar=0.25,
+            in1=halves[:, :, :, CENTRE], op0=ALU.mult, op1=ALU.add,
+        )
+        outer_shape = [P, 2, PLANES, OUTER.stop - OUTER.start]
+        outer_sines = keep.tile(outer_shape, F32)
+        outer_squares = keep.tile(outer_shape, F32)
+        nc.scalar.activation(out=outer_sines[:], in_=halves[:, :, :, OUTER], func=ACT.Sin)
+        nc.scalar.activation(out=outer_squares[:], in_=outer_sines[:], func=ACT.Square)
+        outer_factors = keep.tile(outer_shape, F32)
         nc.vector.tensor_scalar(
-            out=centre_factors[:], in0=centre_squares[:], scalar1=-4.0, scalar2=2.0, op0=ALU.mult, op1=ALU.add
+            out=outer_factors[:], in0=outer_squares[:], scalar1=-4.0, scalar2=2.0, op0=ALU.mult, op1=ALU.add
         )
         k_shape = [P, COILS, PLANES]
         k_re = k_re_bf[:].rearrange("p c g t -> p c (g t)")
         k_im = k_im_bf[:].rearrange("p c g t -> p c (g t)")
-        two_cos, two_sin = (centre_factors[:, i, :].unsqueeze(1).to_broadcast(k_shape) for i in range(2))
+        two_cos, two_sin = (outer_factors[:, i, :, Y_COARSE].unsqueeze(1).to_broadcast(k_shape) for i in range(2))
         kappa_re = keep.tile(k_shape, F32)
         kappa_im = keep.tile(k_shape, F32)
         re_by_cos = keep.tile(k_shape, F32)
@@ -227,33 +228,26 @@ def tile_adjoint_kernel(
         nc.vector.tensor_tensor(out=re_by_sin[:], in0=k_re, in1=two_sin, op=ALU.mult)
         nc.vector.tensor_tensor(out=kappa_re[:], in0=re_by_cos[:], in1=im_by_sin[:], op=ALU.add)
         nc.vector.tensor_tensor(out=kappa_im[:], in0=im_by_cos[:], in1=re_by_sin[:], op=ALU.subtract)
-        diagonal = keep.tile([P, TENSOR_COILS, PLANES, 2, P], F32)
-        for c in range(TENSOR_COILS):
-            for plane in range(PLANES):
-                for term, factor in enumerate((kappa_re, kappa_im)):
-                    nc.scalar.activation(
-                        out=diagonal[:, c, plane, term, :], in_=identity[:], func=ACT.Copy,
-                        scale=factor[:, c, plane : plane + 1],
-                    )
-
-        fine_angles(fine_angle_y, ky)
-        half_shape = [P, PACK, FINE]
-        fine_y_of_pass = wrap_all(
-            nc,
-            tables,
-            [(fine_angle_y[:, g * PACK : (g + 1) * PACK, :], half_shape, 0.0, "fine_y_%d" % g) for g in range(PASSES)],
-        )
+        (fine_y,) = wrap_all(nc, tables, [(fine_angle_y[:], fine_turns_y, fine_shape, 0.0, "fine_y")])
 
         q_x = keep.tile([P, PLANES, 4 * HALF_X], F32)
+        diagonal = keep.tile([P, TENSOR_COILS, PLANES, 2, P], F32)
         for first in range(0, PLANES, GROUP):
             planes = slice(first, first + GROUP)
-            sines_x = stream.tile([P, GROUP, 2 * HALF_X], F32)
+            sines_x = stream.tile([P, GROUP, 2 * HALF_X], F32, bufs=2)
             for i in range(GROUP):
                 half_angle_sines(
                     nc, sines_x[:, i].rearrange("p (w x) -> p w x", w=2), fine_x[:, first + i, :],
-                    half_cos[:, first + i, x_part], half_sin[:, first + i, x_part], X_COARSE,
+                    half_cos[:, first + i, X_PART], half_sin[:, first + i, X_PART], X_COARSE,
                 )
-            squares_x = stream.tile([P, GROUP, 2 * HALF_X], F32)
+            for c in range(TENSOR_COILS):
+                for plane in range(first, first + GROUP):
+                    for term, factor in enumerate((kappa_re, kappa_im)):
+                        nc.scalar.activation(
+                            out=diagonal[:, c, plane, term, :], in_=identity[:], func=ACT.Copy,
+                            scale=factor[:, c, plane : plane + 1],
+                        )
+            squares_x = stream.tile([P, GROUP, 2 * HALF_X], F32, bufs=2)
             nc.vector.tensor_tensor(out=squares_x[:], in0=sines_x[:], in1=sines_x[:], op=ALU.mult)
             nc.vector.tensor_scalar(
                 out=q_x[:, planes, HALF_X : 3 * HALF_X], in0=squares_x[:], scalar1=-1.0, scalar2=0.5,
@@ -376,9 +370,9 @@ def tile_adjoint_kernel(
                     if j in (RE_LOW, IM_LOW):
                         from_view = from_view[:, ::-1, :]
                     if j == IM_LOW:
-                        nc.vector.tensor_scalar(out=to_view, in0=from_view, scalar1=-1.0, scalar2=None, op0=ALU.mult)
+                        nc.scalar.activation(out=to_view, in_=from_view, func=ACT.Copy, scale=-1.0)
                     else:
-                        nc.vector.tensor_copy(out=to_view, in_=from_view)
+                        nc.scalar.copy(out=to_view, in_=from_view)
             grouped_of[c, g] = a_grouped
 
         for c in range(TENSOR_COILS):
@@ -387,42 +381,76 @@ def tile_adjoint_kernel(
             tensor_a(c, 1, sums, ("combined_re_0", "combined_re_1", "combined_im_0", "combined_im_1"))
             quantise_a(c, 1)
 
-        density = keep.tile([P, PLANES], F32)
-        nc.vector.tensor_copy(out=density[:], in_=density_bf[:].rearrange("p o g t -> p (o g t)"))
-        density_minus2 = keep.tile([P, PLANES], F32)
-        nc.vector.tensor_scalar(out=density_minus2[:], in0=density[:], scalar1=-2.0, scalar2=None, op0=ALU.mult)
+        quarter = keep.tile([P, 1], F32)
+        nc.vector.tensor_scalar(
+            out=quarter[:], in0=steps[:, 0:1], scalar1=0.0, scalar2=-0.25 * math.pi, op0=ALU.mult, op1=ALU.add
+        )
+        kappa_y = keep.tile([P, 2, PLANES, Y_COARSE], F32)
+        nc.vector.tensor_tensor(
+            out=kappa_y[:], in0=outer_factors[:, :, :, 0:Y_COARSE],
+            in1=density_bf[:].rearrange("p o g t -> p o (g t)").unsqueeze(3).to_broadcast([P, 2, PLANES, Y_COARSE]),
+            op=ALU.mult,
+        )
+        q_y = keep.tile([P, PLANES, 4 * FINE], F32)
         e_codes = keep.tile([P, PASSES, 3, NY], U32, align_bytes=64)
         e_scales = keep.tile([P, PASSES, 3, NY], U8, align_bytes=64)
         for g in range(PASSES):
-            e_planes = stream.tile([P, PACK, 2, NY], BF16, bufs=2)
+            planes = slice(g * PACK, (g + 1) * PACK)
+            sines_y = stream.tile([P, PACK, 2, FINE], F32, bufs=2)
+            nc.scalar.activation(out=sines_y[:, :, 0, :], in_=fine_y[:, planes, :], func=ACT.Sin, scale=0.5)
+            nc.scalar.activation(
+                out=sines_y[:, :, 1, :], in_=fine_y[:, planes, :], func=ACT.Sin, bias=quarter[:], scale=0.5
+            )
+            squares_y = stream.tile([P, PACK, 2 * FINE], F32, bufs=2)
+            nc.scalar.activation(out=squares_y[:], in_=sines_y[:].rearrange("p t w j -> p t (w j)"), func=ACT.Square)
+            nc.vector.tensor_scalar(
+                out=q_y[:, planes, FINE : 3 * FINE], in0=squares_y[:], scalar1=-1.0, scalar2=0.5,
+                op0=ALU.mult, op1=ALU.add,
+            )
+            nc.vector.tensor_scalar(
+                out=q_y[:, planes, 0:FINE], in0=squares_y[:, :, FINE:], scalar1=-0.5, scalar2=None, op0=ALU.add
+            )
+            nc.vector.tensor_scalar(
+                out=q_y[:, planes, 3 * FINE :], in0=squares_y[:, :, 0:FINE], scalar1=-0.5, scalar2=None, op0=ALU.add
+            )
+            e_planes = stream.tile([P, PACK, Y_COARSE, 4 * FINE], BF16, bufs=2)
             for t in range(PACK):
                 plane = g * PACK + t
-                sines_y = stream.tile([P, 2, NY], F32, bufs=2)
-                half_angle_sines(
-                    nc, sines_y, fine_y_of_pass[g][:, t, :], half_cos[:, plane, y_part], half_sin[:, plane, y_part], Y_COARSE
-                )
-                q_y = stream.tile([P, 2, NY], F32, bufs=2)
-                nc.scalar.activation(out=q_y[:], in_=sines_y[:], func=ACT.Square)
-                nc.vector.tensor_scalar(
-                    out=e_planes[:, t], in0=q_y[:],
-                    scalar1=density_minus2[:, plane : plane + 1], scalar2=density[:, plane : plane + 1],
-                    op0=ALU.mult, op1=ALU.add,
-                )
-            nc.vector.memset(e_planes[:, :, 1, 0:1], 0.0)
+                for n in range(Y_COARSE):
+                    e_terms = stream.tile([P, 2 * FINE], F32, bufs=PACK * Y_COARSE)
+                    nc.scalar.activation(
+                        out=e_terms[:], in_=q_y[:, plane, FINE : 3 * FINE], func=ACT.Copy,
+                        scale=kappa_y[:, 0, plane, n : n + 1],
+                    )
+                    nc.vector.scalar_tensor_tensor(
+                        out=e_planes[:, t, n, :].rearrange("p (s j) -> p s j", s=2),
+                        in0=q_y[:, plane, :].rearrange("p (s j) -> p s j", s=2),
+                        scalar=kappa_y[:, 1, plane, n : n + 1],
+                        in1=e_terms[:].unsqueeze(1).to_broadcast([P, 2, 2 * FINE]),
+                        op0=ALU.mult, op1=ALU.add,
+                    )
             e_grouped = [
                 stream.tile([P, NY, PACK], BF16, name="e_grouped_%d" % kind, tag="grouped", align_bytes=64)
                 for kind in (E_RE, E_IM, E_IM_NEG)
             ]
             for kind in (E_RE, E_IM):
-                to_view, from_view = side_by_side(e_grouped[kind][:], e_planes[:, :, kind, :])
-                nc.vector.tensor_copy(out=to_view, in_=from_view)
+                to_view = e_grouped[kind][:].rearrange("p (n h j) t -> p n h j t", n=Y_COARSE, h=2)
+                blocks = e_planes[:].rearrange("p t n (b j) -> p n b j t", b=4)
+                low = blocks[:, :, 2 + kind, ::-1, :]
+                if kind == E_RE:
+                    nc.scalar.copy(out=to_view[:, :, 1], in_=blocks[:, :, kind])
+                    nc.scalar.copy(out=to_view[:, :, 0], in_=low)
+                else:
+                    nc.vector.tensor_copy(out=to_view[:, :, 1], in_=blocks[:, :, kind])
+                    nc.vector.tensor_scalar(out=to_view[:, :, 0], in0=low, scalar1=-1.0, scalar2=None, op0=ALU.mult)
+            nc.vector.memset(e_grouped[E_IM][:, 0:1, :], 0.0)
             nc.vector.tensor_scalar(
                 out=e_grouped[E_IM_NEG][:], in0=e_grouped[E_IM][:], scalar1=-1.0, scalar2=None, op0=ALU.mult
             )
             for kind in (E_RE, E_IM, E_IM_NEG):
                 quantise(nc, e_grouped[kind][:], e_codes[:, g, kind, :], e_scales[:, g, kind, :])
         table_change = keep.tile([P, 1], F32)
-        nc.scalar.activation(out=table_change[:], in_=q_y[:, 0, 1:2], func=ACT.Sqrt)
+        nc.scalar.activation(out=table_change[:], in_=squares_y[:, PACK - 1, 0:1], func=ACT.Sqrt)
 
         combined_re = [sums.tile([P, NY], F32, name="combined_re_%d" % h) for h in range(X_TILES)]
         combined_im = [sums.tile([P, NY], F32, name="combined_im_%d" % h) for h in range(X_TILES)]
@@ -471,22 +499,27 @@ def tile_adjoint_kernel(
             )
             add_transposed(combined_im[h], re_s_im, False, last_coil)
 
+        early = []
         for c in range(COILS):
             making = c + AHEAD if c + AHEAD < COILS else None
             if making is not None:
                 start_a(making)
-            recons = [recon_matmuls(c, h) for h in range(X_TILES)]
+            recons = early + [recon_matmuls(c, h) for h in range(len(early), X_TILES)]
+            early = []
             if making is not None:
                 finish_a(making)
                 if making + 1 < COILS:
                     gpsimd_a(making + 1)
                 for g in range(PASSES):
                     regroup_a(making, g)
+            between = making == COILS - 1
             for half in range(X_TILES):
                 combine(c, half, recons[half][0], recons[half][1])
-            if making is not None:
-                for g in range(PASSES):
-                    quantise_a(making, g)
+                if making is not None and half == (0 if between else X_TILES - 1):
+                    for g in range(PASSES):
+                        quantise_a(making, g)
+                if between and half == 0:
+                    early = [recon_matmuls(making, 0)]
 
         out_rows = out.rearrange("b x y o -> (b x) (y o)")
         for h in range(X_TILES):
@@ -496,7 +529,7 @@ def tile_adjoint_kernel(
                 blocks = range(piece * Y_BLOCKS // 2, (piece + 1) * Y_BLOCKS // 2)
                 squared = []
                 for name, total in (("re_squared", combined_re[h]), ("im_squared", combined_im[h])):
-                    square = ending.tile([P, NY // 2], F32, name=name, bufs=2)
+                    square = ending.tile([P, NY // 2], F32, name=name, bufs=4)
                     nc.scalar.activation(out=square[:], in_=total[:, cols], func=ACT.Square)
                     squared.append(square)
                 for i, square in enumerate(squared):
@@ -505,6 +538,6 @@ def tile_adjoint_kernel(
                             out=power[:, n * P : (n + 1) * P], lhsT=square[:, n * P : (n + 1) * P], rhs=identity[:],
                             is_transpose=True, start=(i == 0 and n == 0), stop=(i == 1 and n == len(blocks) - 1),
                         )
-                magnitude = ending.tile([P, NY // 2], F32, bufs=2)
+                magnitude = ending.tile([P, NY // 2], F32, bufs=4)
                 nc.scalar.activation(out=magnitude[:], in_=power[:], func=ACT.Sqrt)
                 nc.sync.dma_start(out=out_rows[h * P : (h + 1) * P, cols], in_=magnitude[:])

@@ -24,7 +24,7 @@ FINE = 64
 AHEAD = 1
 TENSOR_COILS = 1
 GROUP = 2
-GPSIMD_SAMPLE = 3
+GPSIMD_PLANES = range(3, PLANES, PACK)
 GPSIMD_FROM = 2
 RUN = 4
 HALF_X = NX // 2
@@ -53,17 +53,19 @@ def by_plane(vector_ap, lead):
 
 
 def wrap_all(nc, pool, jobs):
-    turns = [pool.tile(shape, F32, name="turns_" + label) for angle, given, shape, turn_shift, label in jobs]
+    turns = [
+        pool.tile(shape, F32, name="turns_" + label) if given is None else given
+        for angle, given, shape, turn_shift, label in jobs
+    ]
     wrapped = [pool.tile(shape, F32, name="wrapped_" + label) for angle, given, shape, turn_shift, label in jobs]
     for i, (angle, given, shape, turn_shift, label) in enumerate(jobs):
         if given is None:
             nc.vector.tensor_scalar(
                 out=turns[i][:], in0=angle, scalar1=1.0 / TWO_PI, scalar2=turn_shift, op0=ALU.mult, op1=ALU.add
             )
-    for i, (angle, given, shape, turn_shift, label) in enumerate(jobs):
+    for i in range(len(jobs)):
         nc.vector.tensor_scalar(
-            out=turns[i][:], in0=turns[i][:] if given is None else given[:],
-            scalar1=ROUNDER, scalar2=ROUNDER, op0=ALU.add, op1=ALU.subtract,
+            out=turns[i][:], in0=turns[i][:], scalar1=ROUNDER, scalar2=ROUNDER, op0=ALU.add, op1=ALU.subtract
         )
     for i, (angle, given, shape, turn_shift, label) in enumerate(jobs):
         nc.vector.scalar_tensor_tensor(
@@ -267,35 +269,35 @@ def tile_adjoint_kernel(
 
         def gpsimd_a(c):
             start_planes(c)
-            firsts = stream.tile([P, PASSES, NX], F32, bufs=1)
-            seconds = stream.tile([P, PASSES, NX], F32, tag="last_terms", bufs=1)
-            for g in range(PASSES):
-                plane = g * PACK + GPSIMD_SAMPLE
+            count = len(GPSIMD_PLANES)
+            firsts = stream.tile([P, count, NX], F32, bufs=1)
+            seconds = stream.tile([P, count, 2 * NX], F32, bufs=1)
+            for i, plane in enumerate(GPSIMD_PLANES):
                 nc.scalar.activation(
-                    out=firsts[:, g, :], in_=q_x[:, plane, HALF_X : 3 * HALF_X], func=ACT.Copy,
+                    out=firsts[:, i, :], in_=q_x[:, plane, HALF_X : 3 * HALF_X], func=ACT.Copy,
                     scale=kappa_re[:, c, plane : plane + 1],
                 )
-            for g in range(PASSES):
-                plane = g * PACK + GPSIMD_SAMPLE
                 nc.scalar.activation(
-                    out=seconds[:, g, :], in_=q_x[:, plane, 0 : 2 * HALF_X], func=ACT.Copy,
+                    out=seconds[:, i, :], in_=q_x[:, plane, :], func=ACT.Copy,
                     scale=kappa_im[:, c, plane : plane + 1],
                 )
-            for op, cols in ((ALU.add, slice(0, NX)), (ALU.subtract, slice(NX, 2 * NX))):
-                nc.gpsimd.tensor_tensor(
-                    out=planes_of[c][:, :, GPSIMD_SAMPLE, cols], in0=firsts[:], in1=seconds[:], op=op
-                )
+            by_number = planes_of[c][:].rearrange("p g t x -> p (g t) x")
+            sums_view = by_number[:, GPSIMD_PLANES.start : GPSIMD_PLANES.stop : GPSIMD_PLANES.step, :]
+            g, t = divmod(vector_planes(c - 1)[-1], PACK)
+            nc.gpsimd.tensor_copy(out=sums_view[:, 0, 0:1], in_=planes_of[c - 1][:, g, t, 0:1])
+            nc.gpsimd.tensor_tensor(
+                out=sums_view.rearrange("p n (s x) -> p n s x", s=2),
+                in0=firsts[:].unsqueeze(2).to_broadcast([P, count, 2, NX]),
+                in1=seconds[:].rearrange("p n (s x) -> p n s x", s=2),
+                op=ALU.add,
+            )
 
         def vector_planes(c):
-            return [p for p in range(PLANES) if c < GPSIMD_FROM or p % PACK != GPSIMD_SAMPLE]
+            return [p for p in range(PLANES) if c < GPSIMD_FROM or p not in GPSIMD_PLANES]
 
         def start_a(c):
-            planes = vector_planes(c)
-            for plane in planes:
-                if plane == planes[-1]:
-                    first_terms = stream.tile([P, NX], F32, name="last_terms", tag="last_terms", bufs=1)
-                else:
-                    first_terms = stream.tile([P, NX], F32, bufs=PLANES - 1)
+            for plane in vector_planes(c):
+                first_terms = stream.tile([P, NX], F32, bufs=PLANES)
                 nc.scalar.activation(
                     out=first_terms[:], in_=q_x[:, plane, HALF_X : 3 * HALF_X], func=ACT.Copy,
                     scale=kappa_re[:, c, plane : plane + 1],
@@ -316,7 +318,7 @@ def tile_adjoint_kernel(
                 )
 
         def regroup_a(c, g):
-            a_grouped = stream.tile([P, 2 * NX, PACK], BF16, tag="grouped", align_bytes=64)
+            a_grouped = stream.tile([P, 2 * NX, PACK], BF16, tag="grouped", align_bytes=64, bufs=5)
             a_planes = planes_of[c][:, g]
             to_view, from_view = side_by_side(a_grouped[:, 0:NX], a_planes[:, :, 0:NX])
             nc.scalar.copy(out=to_view, in_=from_view)
@@ -355,7 +357,7 @@ def tile_adjoint_kernel(
                 order = [(t, j) for t in range(PACK) for j in banks]
             else:
                 order = [(t, j) for j in banks for t in range(PACK)]
-            a_grouped = stream.tile([P, 2 * NX, PACK], BF16, tag="grouped", align_bytes=64)
+            a_grouped = stream.tile([P, 2 * NX, PACK], BF16, tag="grouped", align_bytes=64, bufs=5)
             for t, j in order:
                 plane = g * PACK + t
                 for term, block in enumerate((1 + j % 2, j)):
@@ -377,9 +379,7 @@ def tile_adjoint_kernel(
 
         for c in range(TENSOR_COILS):
             tensor_a(c, 0, recon, ("recon_re", "recon_im", "recon_re", "recon_im"))
-            quantise_a(c, 0)
             tensor_a(c, 1, sums, ("combined_re_0", "combined_re_1", "combined_im_0", "combined_im_1"))
-            quantise_a(c, 1)
 
         quarter = keep.tile([P, 1], F32)
         nc.vector.tensor_scalar(
@@ -430,7 +430,7 @@ def tile_adjoint_kernel(
                         op0=ALU.mult, op1=ALU.add,
                     )
             e_grouped = [
-                stream.tile([P, NY, PACK], BF16, name="e_grouped_%d" % kind, tag="grouped", align_bytes=64)
+                stream.tile([P, NY, PACK], BF16, name="e_grouped_%d" % kind, tag="grouped", align_bytes=64, bufs=5)
                 for kind in (E_RE, E_IM, E_IM_NEG)
             ]
             for kind in (E_RE, E_IM):
@@ -447,6 +447,8 @@ def tile_adjoint_kernel(
             nc.vector.tensor_scalar(
                 out=e_grouped[E_IM_NEG][:], in0=e_grouped[E_IM][:], scalar1=-1.0, scalar2=None, op0=ALU.mult
             )
+            for c in range(TENSOR_COILS):
+                quantise_a(c, g)
             for kind in (E_RE, E_IM, E_IM_NEG):
                 quantise(nc, e_grouped[kind][:], e_codes[:, g, kind, :], e_scales[:, g, kind, :])
         table_change = keep.tile([P, 1], F32)
@@ -484,16 +486,16 @@ def tile_adjoint_kernel(
         def combine(c, h, recon_re, recon_im):
             s_re, s_im = maps_re[:, c, h, :], maps_im[:, c, h, :]
             first_coil, last_coil = c == 0, c == COILS - 1
-            re_s_re = stream.tile([P, NY], F32)
+            re_s_re = stream.tile([P, NY], F32, bufs=2)
             nc.vector.tensor_tensor(out=re_s_re[:], in0=recon_re[:], in1=s_re, op=ALU.mult)
             add_transposed(combined_re[h], re_s_re, first_coil, False)
-            im_s_im = stream.tile([P, NY], F32)
+            im_s_im = stream.tile([P, NY], F32, bufs=2)
             nc.vector.tensor_tensor(out=im_s_im[:], in0=recon_im[:], in1=s_im, op=ALU.mult)
             add_transposed(combined_re[h], im_s_im, False, last_coil)
-            im_s_re = stream.tile([P, NY], F32)
+            im_s_re = stream.tile([P, NY], F32, bufs=2)
             nc.vector.tensor_tensor(out=im_s_re[:], in0=recon_im[:], in1=s_re, op=ALU.mult)
             add_transposed(combined_im[h], im_s_re, first_coil, False)
-            re_s_im = stream.tile([P, NY], F32)
+            re_s_im = stream.tile([P, NY], F32, bufs=2)
             nc.vector.scalar_tensor_tensor(
                 out=re_s_im[:], in0=recon_re[:], scalar=-1.0, in1=s_im, op0=ALU.mult, op1=ALU.mult
             )

@@ -24,7 +24,7 @@ FINE = 64
 AHEAD = 1
 TENSOR_COILS = 1
 GROUP = 2
-GPSIMD_PLANES = range(3, PLANES, PACK)
+GPSIMD_PLANES = range(3, PLANES, 2)
 GPSIMD_FROM = 2
 RUN = 4
 HALF_X = NX // 2
@@ -271,26 +271,22 @@ def tile_adjoint_kernel(
             start_planes(c)
             count = len(GPSIMD_PLANES)
             firsts = stream.tile([P, count, NX], F32, bufs=1)
-            seconds = stream.tile([P, count, 2 * NX], F32, bufs=1)
+            seconds = stream.tile([P, count, NX], F32, bufs=1)
             for i, plane in enumerate(GPSIMD_PLANES):
                 nc.scalar.activation(
                     out=firsts[:, i, :], in_=q_x[:, plane, HALF_X : 3 * HALF_X], func=ACT.Copy,
                     scale=kappa_re[:, c, plane : plane + 1],
                 )
                 nc.scalar.activation(
-                    out=seconds[:, i, :], in_=q_x[:, plane, :], func=ACT.Copy,
+                    out=seconds[:, i, :], in_=q_x[:, plane, 0:NX], func=ACT.Copy,
                     scale=kappa_im[:, c, plane : plane + 1],
                 )
             by_number = planes_of[c][:].rearrange("p g t x -> p (g t) x")
             sums_view = by_number[:, GPSIMD_PLANES.start : GPSIMD_PLANES.stop : GPSIMD_PLANES.step, :]
             g, t = divmod(vector_planes(c - 1)[-1], PACK)
             nc.gpsimd.tensor_copy(out=sums_view[:, 0, 0:1], in_=planes_of[c - 1][:, g, t, 0:1])
-            nc.gpsimd.tensor_tensor(
-                out=sums_view.rearrange("p n (s x) -> p n s x", s=2),
-                in0=firsts[:].unsqueeze(2).to_broadcast([P, count, 2, NX]),
-                in1=seconds[:].rearrange("p n (s x) -> p n s x", s=2),
-                op=ALU.add,
-            )
+            for op, cols in ((ALU.add, slice(0, NX)), (ALU.subtract, slice(NX, 2 * NX))):
+                nc.gpsimd.tensor_tensor(out=sums_view[:, :, cols], in0=firsts[:], in1=seconds[:], op=op)
 
         def vector_planes(c):
             return [p for p in range(PLANES) if c < GPSIMD_FROM or p not in GPSIMD_PLANES]
@@ -461,9 +457,9 @@ def tile_adjoint_kernel(
             a_re, a_im = (RE_LOW, IM_LOW) if h == 0 else (RE_HIGH, IM_HIGH)
             recon_re = recon.tile([P, NY], F32)
             recon_im = recon.tile([P, NY], F32)
-            for g in range(PASSES):
-                for block, kind_for_re, kind_for_im in ((a_re, E_RE, E_IM), (a_im, E_IM_NEG, E_RE)):
-                    for acc, kind in ((recon_re, kind_for_re), (recon_im, kind_for_im)):
+            for acc, kind_for_a_re, kind_for_a_im in ((recon_re, E_RE, E_IM_NEG), (recon_im, E_IM, E_RE)):
+                for g in range(PASSES):
+                    for block, kind in ((a_re, kind_for_a_re), (a_im, kind_for_a_im)):
                         nc.tensor.matmul_mx(
                             out=acc[:],
                             lhsT=a_codes[:, g, block, :].bitcast(FP8X4),
@@ -489,17 +485,17 @@ def tile_adjoint_kernel(
             re_s_re = stream.tile([P, NY], F32, bufs=2)
             nc.vector.tensor_tensor(out=re_s_re[:], in0=recon_re[:], in1=s_re, op=ALU.mult)
             add_transposed(combined_re[h], re_s_re, first_coil, False)
+            re_s_im = stream.tile([P, NY], F32, bufs=2)
+            nc.vector.scalar_tensor_tensor(
+                out=re_s_im[:], in0=recon_re[:], scalar=-1.0, in1=s_im, op0=ALU.mult, op1=ALU.mult
+            )
+            add_transposed(combined_im[h], re_s_im, first_coil, False)
             im_s_im = stream.tile([P, NY], F32, bufs=2)
             nc.vector.tensor_tensor(out=im_s_im[:], in0=recon_im[:], in1=s_im, op=ALU.mult)
             add_transposed(combined_re[h], im_s_im, False, last_coil)
             im_s_re = stream.tile([P, NY], F32, bufs=2)
             nc.vector.tensor_tensor(out=im_s_re[:], in0=recon_im[:], in1=s_re, op=ALU.mult)
-            add_transposed(combined_im[h], im_s_re, first_coil, False)
-            re_s_im = stream.tile([P, NY], F32, bufs=2)
-            nc.vector.scalar_tensor_tensor(
-                out=re_s_im[:], in0=recon_re[:], scalar=-1.0, in1=s_im, op0=ALU.mult, op1=ALU.mult
-            )
-            add_transposed(combined_im[h], re_s_im, False, last_coil)
+            add_transposed(combined_im[h], im_s_re, False, last_coil)
 
         early = []
         for c in range(COILS):

@@ -284,7 +284,7 @@ def tile_adjoint_kernel(
             by_number = planes_of[c][:].rearrange("p g t x -> p (g t) x")
             sums_view = by_number[:, GPSIMD_PLANES.start : GPSIMD_PLANES.stop : GPSIMD_PLANES.step, :]
             g, t = divmod(vector_planes(c - 1)[-1], PACK)
-            nc.gpsimd.tensor_copy(out=sums_view[:, 0, 0:1], in_=planes_of[c - 1][:, g, t, 0:1])
+            nc.gpsimd.tensor_copy(out=sums_view[:, 0, 0 : 2 * NX : NX], in_=planes_of[c - 1][:, g, t, 0 : 2 * NX : NX])
             for op, cols in ((ALU.add, slice(0, NX)), (ALU.subtract, slice(NX, 2 * NX))):
                 nc.gpsimd.tensor_tensor(out=sums_view[:, :, cols], in0=firsts[:], in1=seconds[:], op=op)
 

@@ -43,7 +43,7 @@ TWO_PI_LOW = TWO_PI - TWO_PI_HIGH
 ROUNDER = 1.5 * 2.0**23
 
 E_RE, E_IM, E_IM_NEG = 0, 1, 2
-RE_HIGH, IM_HIGH, RE_LOW, IM_LOW = 0, 1, 2, 3
+RE_HIGH, IM_HIGH, IM_LOW_NEG, RE_LOW = 0, 1, 2, 3
 
 FLOPS = 4 * 2 * COILS * NX * SAMPLES * NY
 
@@ -318,13 +318,8 @@ def tile_adjoint_kernel(
             a_planes = planes_of[c][:, g]
             to_view, from_view = side_by_side(a_grouped[:, 0:NX], a_planes[:, :, 0:NX])
             nc.scalar.copy(out=to_view, in_=from_view)
-            for block in (RE_LOW, IM_LOW):
-                cols = slice(block * HALF_X, (block + 1) * HALF_X)
-                to_view, from_view = side_by_side(a_grouped[:, cols], a_planes[:, :, cols][:, :, ::-1])
-                if block == RE_LOW:
-                    nc.scalar.copy(out=to_view, in_=from_view)
-                else:
-                    nc.scalar.activation(out=to_view, in_=from_view, func=ACT.Copy, scale=-1.0)
+            to_view, from_view = side_by_side(a_grouped[:, NX:], a_planes[:, :, NX:][:, :, ::-1])
+            nc.scalar.copy(out=to_view, in_=from_view)
             grouped_of[c, g] = a_grouped
 
         def quantise_a(c, g):
@@ -363,14 +358,11 @@ def tile_adjoint_kernel(
                         start=(t == 0 and term == 0), stop=(t == PACK - 1 and term == 1),
                     )
                 if t == PACK - 1:
-                    to_view = a_grouped[:, j * P : (j + 1) * P, :]
+                    block = (RE_HIGH, IM_HIGH, RE_LOW, IM_LOW_NEG)[j]
                     from_view = a_sums[j][:].rearrange("p t x -> p x t")
-                    if j in (RE_LOW, IM_LOW):
+                    if block in (RE_LOW, IM_LOW_NEG):
                         from_view = from_view[:, ::-1, :]
-                    if j == IM_LOW:
-                        nc.scalar.activation(out=to_view, in_=from_view, func=ACT.Copy, scale=-1.0)
-                    else:
-                        nc.scalar.copy(out=to_view, in_=from_view)
+                    nc.scalar.copy(out=a_grouped[:, block * P : (block + 1) * P, :], in_=from_view)
             grouped_of[c, g] = a_grouped
 
         for c in range(TENSOR_COILS):
@@ -443,8 +435,10 @@ def tile_adjoint_kernel(
             nc.vector.tensor_scalar(
                 out=e_grouped[E_IM_NEG][:], in0=e_grouped[E_IM][:], scalar1=-1.0, scalar2=None, op0=ALU.mult
             )
-            for c in range(TENSOR_COILS):
-                quantise_a(c, g)
+            if g == PASSES - 1:
+                for c in range(TENSOR_COILS):
+                    for a_pass in range(PASSES):
+                        quantise_a(c, a_pass)
             for kind in (E_RE, E_IM, E_IM_NEG):
                 quantise(nc, e_grouped[kind][:], e_codes[:, g, kind, :], e_scales[:, g, kind, :])
         table_change = keep.tile([P, 1], F32)
@@ -454,20 +448,25 @@ def tile_adjoint_kernel(
         combined_im = [sums.tile([P, NY], F32, name="combined_im_%d" % h) for h in range(X_TILES)]
         def recon_matmuls(c, h):
             a_codes, a_scales = words_of[c]
-            a_re, a_im = (RE_LOW, IM_LOW) if h == 0 else (RE_HIGH, IM_HIGH)
+            if h == 0:
+                re_terms = ((RE_LOW, E_RE), (IM_LOW_NEG, E_IM))
+                im_terms = ((RE_LOW, E_IM_NEG), (IM_LOW_NEG, E_RE))
+            else:
+                re_terms = ((RE_HIGH, E_RE), (IM_HIGH, E_IM_NEG))
+                im_terms = ((RE_HIGH, E_IM), (IM_HIGH, E_RE))
             recon_re = recon.tile([P, NY], F32)
             recon_im = recon.tile([P, NY], F32)
-            for acc, kind_for_a_re, kind_for_a_im in ((recon_re, E_RE, E_IM_NEG), (recon_im, E_IM, E_RE)):
+            for acc, terms in ((recon_re, re_terms), (recon_im, im_terms)):
                 for g in range(PASSES):
-                    for block, kind in ((a_re, kind_for_a_re), (a_im, kind_for_a_im)):
+                    for i, (block, kind) in enumerate(terms):
                         nc.tensor.matmul_mx(
                             out=acc[:],
                             lhsT=a_codes[:, g, block, :].bitcast(FP8X4),
                             lhsT_scale=a_scales[:, g, block, :],
                             rhs=e_codes[:, g, kind, :].bitcast(FP8X4),
                             rhs_scale=e_scales[:, g, kind, :],
-                            start=(g == 0 and block == a_re),
-                            stop=(g == PASSES - 1 and block == a_im),
+                            start=(g == 0 and i == 0),
+                            stop=(g == PASSES - 1 and i == 1),
                         )
             return recon_re, recon_im
 
@@ -482,16 +481,23 @@ def tile_adjoint_kernel(
         def combine(c, h, recon_re, recon_im):
             s_re, s_im = maps_re[:, c, h, :], maps_im[:, c, h, :]
             first_coil, last_coil = c == 0, c == COILS - 1
+
+            def times_s_im(out, factor, negated):
+                if negated:
+                    nc.vector.scalar_tensor_tensor(
+                        out=out[:], in0=factor[:], scalar=-1.0, in1=s_im, op0=ALU.mult, op1=ALU.mult
+                    )
+                else:
+                    nc.vector.tensor_tensor(out=out[:], in0=factor[:], in1=s_im, op=ALU.mult)
+
             re_s_re = stream.tile([P, NY], F32, bufs=2)
             nc.vector.tensor_tensor(out=re_s_re[:], in0=recon_re[:], in1=s_re, op=ALU.mult)
             add_transposed(combined_re[h], re_s_re, first_coil, False)
             re_s_im = stream.tile([P, NY], F32, bufs=2)
-            nc.vector.scalar_tensor_tensor(
-                out=re_s_im[:], in0=recon_re[:], scalar=-1.0, in1=s_im, op0=ALU.mult, op1=ALU.mult
-            )
+            times_s_im(re_s_im, recon_re, h == 1)
             add_transposed(combined_im[h], re_s_im, first_coil, False)
             im_s_im = stream.tile([P, NY], F32, bufs=2)
-            nc.vector.tensor_tensor(out=im_s_im[:], in0=recon_im[:], in1=s_im, op=ALU.mult)
+            times_s_im(im_s_im, recon_im, h == 0)
             add_transposed(combined_re[h], im_s_im, False, last_coil)
             im_s_re = stream.tile([P, NY], F32, bufs=2)
             nc.vector.tensor_tensor(out=im_s_re[:], in0=recon_im[:], in1=s_re, op=ALU.mult)

import math

import concourse.mybir as mybir
from concourse.masks import make_identity

F32 = mybir.dt.float32
BF16 = mybir.dt.bfloat16
U8 = mybir.dt.uint8
U32 = mybir.dt.uint32
FP8X4 = mybir.dt.float8_e4m3fn_x4
ALU = mybir.AluOpType
ACT = mybir.ActivationFunctionType

P = 128
PACK = 4
K_PASS = P * PACK

COILS, SAMPLES, NX, NY = 8, 1024, 256, 512
PASSES = SAMPLES // K_PASS
PLANES = PASSES * PACK
X_TILES = NX // P
assert X_TILES == PASSES
FINE = 64
AHEAD = 1
TENSOR_COILS = 1
GROUP = 2
GPSIMD_PLANES = range(3, PLANES, 2)
GPSIMD_FROM = 2
RUN = 4
HALF_X = NX // 2
X_COARSE = HALF_X // FINE
Y_SPAN = 2 * FINE
Y_COARSE = NY // Y_SPAN
X_PART, Y_PART = slice(0, X_COARSE), slice(X_COARSE, X_COARSE + Y_COARSE)
CENTRE = X_COARSE + Y_COARSE
N_COARSE = CENTRE + 1
OUTER = slice(X_COARSE, N_COARSE)
Y_BLOCKS = NY // P

TWO_PI = 2.0 * math.pi
TWO_PI_HIGH = round(TWO_PI * 4096.0) / 4096.0
TWO_PI_LOW = TWO_PI - TWO_PI_HIGH
ROUNDER = 1.5 * 2.0**23

E_RE, E_IM, E_IM_NEG = 0, 1, 2
RE_HIGH, IM_HIGH, IM_LOW_NEG, RE_LOW = 0, 1, 2, 3

FLOPS = 4 * 2 * COILS * NX * SAMPLES * NY


def by_plane(vector_ap, lead):
    return vector_ap.rearrange(lead + " (g p t) -> p " + lead + " g t", g=PASSES, p=P, t=PACK)


def wrap_all(nc, pool, jobs):
    turns = [
        pool.tile(shape, F32, name="turns_" + label) if given is None else given
        for angle, given, shape, turn_shift, label in jobs
    ]
    wrapped = [pool.tile(shape, F32, name="wrapped_" + label) for angle, given, shape, turn_shift, label in jobs]
    for i, (angle, given, shape, turn_shift, label) in enumerate(jobs):
        if given is None:
            nc.vector.tensor_scalar(
                out=turns[i][:], in0=angle, scalar1=1.0 / TWO_PI, scalar2=turn_shift, op0=ALU.mult, op1=ALU.add
            )
    for i in range(len(jobs)):
        nc.vector.tensor_scalar(
            out=turns[i][:], in0=turns[i][:], scalar1=ROUNDER, scalar2=ROUNDER, op0=ALU.add, op1=ALU.subtract
        )
    for i, (angle, given, shape, turn_shift, label) in enumerate(jobs):
        nc.vector.scalar_tensor_tensor(
            out=wrapped[i][:], in0=turns[i][:], scalar=-TWO_PI_HIGH, in1=angle, op0=ALU.mult, op1=ALU.add
        )
    for i in range(len(jobs)):
        nc.vector.scalar_tensor_tensor(
            out=wrapped[i][:], in0=turns[i][:], scalar=-TWO_PI_LOW, in1=wrapped[i][:], op0=ALU.mult, op1=ALU.add
        )
    return wrapped


def half_angle_sines(nc, out, fine, half_cos, half_sin, n_coarse):
    for which, half in enumerate((half_cos, half_sin)):
        for coarse in range(n_coarse):
            nc.scalar.activation(
                out=out[:, which, coarse * FINE : (coarse + 1) * FINE],
                in_=fine,
                func=ACT.Sin,
                bias=half[:, coarse : coarse + 1],
                scale=0.5,
            )


def side_by_side(grouped, planes):
    return (
        grouped.rearrange("p (w i) t -> p w t i", i=RUN),
        planes.rearrange("p t (w i) -> p w t i", i=RUN),
    )


def quantise(nc, grouped, codes, scales):
    nc.vector.quantize_mx(
        out=codes.bitcast(FP8X4), scales=scales, in_=grouped.rearrange("p w t -> p (w t)")
    )


def tile_adjoint_kernel(
    tc, kspace_real, kspace_imag, trajectory, smaps_real, smaps_imag, density_comp, out
):
    nc = tc.nc
    with (
        tc.tile_pool(name="keep", bufs=1) as keep,
        tc.tile_pool(name="tables", bufs=1) as tables,
        tc.tile_pool(name="stream", bufs=3) as stream,
        tc.tile_pool(name="coil", bufs=3) as coil_pool,
        tc.tile_pool(name="ending", bufs=1) as ending,
        tc.psum_pool(name="sums", bufs=1) as sums,
        tc.psum_pool(name="recon", bufs=2) as recon,
    ):
        traj_bf = keep.tile([P, 2, PASSES, PACK], BF16)
        nc.sync.dma_start(out=traj_bf[:], in_=by_plane(trajectory, "a"))
        density_bf = keep.tile([P, 1, PASSES, PACK], BF16)
        nc.sync.dma_start(out=density_bf[:], in_=by_plane(density_comp.rearrange("(o m) -> o m", o=1), "o"))
        k_re_bf = keep.tile([P, COILS, PASSES, PACK], BF16)
        nc.sync.dma_start(out=k_re_bf[:], in_=by_plane(kspace_real.rearrange("b c m -> (b c) m"), "c"))
        k_im_bf = keep.tile([P, COILS, PASSES, PACK], BF16)
        nc.sync.dma_start(out=k_im_bf[:], in_=by_plane(kspace_imag.rearrange("b c m -> (b c) m"), "c"))

        maps_re = keep.tile([P, COILS, X_TILES, NY], BF16)
        maps_im = keep.tile([P, COILS, X_TILES, NY], BF16)
        maps_re_dram = smaps_real.rearrange("b c (h p) y -> p (b c) h y", p=P)
        maps_im_dram = smaps_imag.rearrange("b c (h p) y -> p (b c) h y", p=P)
        for c in range(COILS):
            nc.sync.dma_start(out=maps_re[:, c], in_=maps_re_dram[:, c])
            nc.sync.dma_start(out=maps_im[:, c], in_=maps_im_dram[:, c])

        steps = keep.tile([P, FINE], F32)
        nc.gpsimd.iota(
            out=steps[:], pattern=[[1, FINE]], base=0, channel_multiplier=0,
            allow_small_or_imprecise_dtypes=True,
        )
        nc.gpsimd.tensor_scalar(out=steps[:], in0=steps[:], scalar1=0.5, scalar2=None, op0=ALU.add)
        starts = keep.tile([P, N_COARSE], F32)
        nc.gpsimd.iota(
            out=starts[:, X_PART], pattern=[[FINE, X_COARSE]], base=0, channel_multiplier=0,
            allow_small_or_imprecise_dtypes=True,
        )
        nc.gpsimd.iota(
            out=starts[:, Y_PART], pattern=[[Y_SPAN, Y_COARSE]], base=FINE, channel_multiplier=0,
            allow_small_or_imprecise_dtypes=True,
        )
        nc.gpsimd.tensor_scalar(
            out=starts[:, Y_PART], in0=starts[:, Y_PART], scalar1=-0.5, scalar2=None, op0=ALU.add
        )
        nc.gpsimd.iota(
            out=starts[:, CENTRE : CENTRE + 1], pattern=[[1, 1]], base=NY // 2, channel_multiplier=0,
            allow_small_or_imprecise_dtypes=True,
        )
        identity = keep.tile([P, P], F32)
        make_identity(nc, identity[:])
        first_sine = keep.tile([P, 1], F32)
        nc.scalar.activation(out=first_sine[:], in_=steps[:, 0:1], func=ACT.Sin)

        traj = keep.tile([P, 2, PLANES], F32)
        nc.vector.tensor_copy(out=traj[:], in_=traj_bf[:].rearrange("p a g t -> p a (g t)"))
        kx, ky = traj[:, 0, :], traj[:, 1, :]
        fine_shape = [P, PLANES, FINE]
        fine_angle_x = tables.tile(fine_shape, F32)
        fine_angle_y = tables.tile(fine_shape, F32)

        fine_turns_x = tables.tile(fine_shape, F32)
        fine_turns_y = tables.tile(fine_shape, F32)
        for fine_angle, fine_turns, rate in ((fine_angle_x, fine_turns_x, kx), (fine_angle_y, fine_turns_y, ky)):
            for plane in range(PLANES):
                nc.scalar.activation(
                    out=fine_angle[:, plane, :], in_=steps[:], func=ACT.Copy, scale=rate[:, plane : plane + 1]
                )
            nc.scalar.activation(out=fine_turns[:], in_=fine_angle[:], func=ACT.Copy, scale=1.0 / TWO_PI)

        coarse_shape = [P, PLANES, N_COARSE]
        coarse_angle = tables.tile(coarse_shape, F32)
        for part, rate in ((X_PART, kx), (OUTER, ky)):
            shape = [P, PLANES, part.stop - part.start]
            nc.vector.tensor_tensor(
                out=coarse_angle[:, :, part],
                in0=rate.unsqueeze(2).to_broadcast(shape),
                in1=starts[:, part].unsqueeze(1).to_broadcast(shape),
                op=ALU.mult,
            )
        fine_x, for_cos, for_sin = wrap_all(
            nc,
            tables,
            (
                (fine_angle_x[:], fine_turns_x, fine_shape, 0.0, "fine_x"),
                (coarse_angle[:], None, coarse_shape, 0.0, "cos"),
                (coarse_angle[:], None, coarse_shape, -0.25, "sin"),
            ),
        )
        halves = tables.tile([P, 2] + coarse_shape[1:], F32)
        half_cos, half_sin = halves[:, 0], halves[:, 1]
        nc.vector.tensor_scalar(out=half_cos, in0=for_cos[:], scalar1=0.5, scalar2=None, op0=ALU.mult)
        nc.vector.tensor_scalar(
            out=half_sin, in0=for_sin[:], scalar1=-0.5 * math.pi, scalar2=0.5, op0=ALU.add, op1=ALU.mult
        )
        nc.vector.scalar_tensor_tensor(
            out=halves[:, :, :, CENTRE], in0=kx.unsqueeze(1).to_broadcast([P, 2, PLANES]), scalar=0.25,
            in1=halves[:, :, :, CENTRE], op0=ALU.mult, op1=ALU.add,
        )
        outer_shape = [P, 2, PLANES, OUTER.stop - OUTER.start]
        outer_sines = keep.tile(outer_shape, F32)
        outer_squares = keep.tile(outer_shape, F32)
        nc.scalar.activation(out=outer_sines[:], in_=halves[:, :, :, OUTER], func=ACT.Sin)
        nc.scalar.activation(out=outer_squares[:], in_=outer_sines[:], func=ACT.Square)
        outer_factors = keep.tile(outer_shape, F32)
        nc.vector.tensor_scalar(
            out=outer_factors[:], in0=outer_squares[:], scalar1=-4.0, scalar2=2.0, op0=ALU.mult, op1=ALU.add
        )
        k_shape = [P, COILS, PLANES]
        k_re = k_re_bf[:].rearrange("p c g t -> p c (g t)")
        k_im = k_im_bf[:].rearrange("p c g t -> p c (g t)")
        two_cos, two_sin = (outer_factors[:, i, :, Y_COARSE].unsqueeze(1).to_broadcast(k_shape) for i in range(2))
        kappa_re = keep.tile(k_shape, F32)
        kappa_im = keep.tile(k_shape, F32)
        re_by_cos = keep.tile(k_shape, F32)
        im_by_sin = keep.tile(k_shape, F32)
        im_by_cos = keep.tile(k_shape, F32)
        re_by_sin = keep.tile(k_shape, F32)
        nc.vector.tensor_tensor(out=re_by_cos[:], in0=k_re, in1=two_cos, op=ALU.mult)
        nc.vector.tensor_tensor(out=im_by_sin[:], in0=k_im, in1=two_sin, op=ALU.mult)
        nc.vector.tensor_tensor(out=im_by_cos[:], in0=k_im, in1=two_cos, op=ALU.mult)
        nc.vector.tensor_tensor(out=re_by_sin[:], in0=k_re, in1=two_sin, op=ALU.mult)
        nc.vector.tensor_tensor(out=kappa_re[:], in0=re_by_cos[:], in1=im_by_sin[:], op=ALU.add)
        nc.vector.tensor_tensor(out=kappa_im[:], in0=im_by_cos[:], in1=re_by_sin[:], op=ALU.subtract)
        (fine_y,) = wrap_all(nc, tables, [(fine_angle_y[:], fine_turns_y, fine_shape, 0.0, "fine_y")])

        q_x = keep.tile([P, PLANES, 4 * HALF_X], F32)
        diagonal = keep.tile([P, TENSOR_COILS, PLANES, 2, P], F32)
        for first in range(0, PLANES, GROUP):
            planes = slice(first, first + GROUP)
            sines_x = stream.tile([P, GROUP, 2 * HALF_X], F32, bufs=2)
            for i in range(GROUP):
                half_angle_sines(
                    nc, sines_x[:, i].rearrange("p (w x) -> p w x", w=2), fine_x[:, first + i, :],
                    half_cos[:, first + i, X_PART], half_sin[:, first + i, X_PART], X_COARSE,
                )
            for c in range(TENSOR_COILS):
                for plane in range(first, first + GROUP):
                    for term, factor in enumerate((kappa_re, kappa_im)):
                        nc.scalar.activation(
                            out=diagonal[:, c, plane, term, :], in_=identity[:], func=ACT.Copy,
                            scale=factor[:, c, plane : plane + 1],
                        )
            squares_x = stream.tile([P, GROUP, 2 * HALF_X], F32, bufs=2)
            nc.vector.tensor_tensor(out=squares_x[:], in0=sines_x[:], in1=sines_x[:], op=ALU.mult)
            nc.vector.tensor_scalar(
                out=q_x[:, planes, HALF_X : 3 * HALF_X], in0=squares_x[:], scalar1=-1.0, scalar2=0.5,
                op0=ALU.mult, op1=ALU.add,
            )
            nc.vector.tensor_scalar(
                out=q_x[:, planes, 0:HALF_X], in0=squares_x[:, :, HALF_X:], scalar1=-0.5, scalar2=None, op0=ALU.add
            )
            nc.vector.tensor_scalar(
                out=q_x[:, planes, 3 * HALF_X :], in0=squares_x[:, :, 0:HALF_X], scalar1=-0.5, scalar2=None, op0=ALU.add
            )

        terms_of, planes_of, grouped_of, words_of = {}, {}, {}, {}

        def start_planes(c):
            planes_of[c] = stream.tile([P, PASSES, PACK, 2 * NX], BF16, name="a_planes")

        def gpsimd_a(c):
            start_planes(c)
            count = len(GPSIMD_PLANES)
            firsts = stream.tile([P, count, NX], F32, bufs=1)
            seconds = stream.tile([P, count, NX], F32, bufs=1)
            for i, plane in enumerate(GPSIMD_PLANES):
                nc.scalar.activation(
                    out=firsts[:, i, :], in_=q_x[:, plane, HALF_X : 3 * HALF_X], func=ACT.Copy,
                    scale=kappa_re[:, c, plane : plane + 1],
                )
                nc.scalar.activation(
                    out=seconds[:, i, :], in_=q_x[:, plane, 0:NX], func=ACT.Copy,
                    scale=kappa_im[:, c, plane : plane + 1],
                )
            by_number = planes_of[c][:].rearrange("p g t x -> p (g t) x")
            sums_view = by_number[:, GPSIMD_PLANES.start : GPSIMD_PLANES.stop : GPSIMD_PLANES.step, :]
            g, t = divmod(vector_planes(c - 1)[-1], PACK)
            nc.gpsimd.tensor_copy(out=sums_view[:, 0, 0 : 2 * NX : NX], in_=planes_of[c - 1][:, g, t, 0 : 2 * NX : NX])
            for op, cols in ((ALU.add, slice(0, NX)), (ALU.subtract, slice(NX, 2 * NX))):
                nc.gpsimd.tensor_tensor(out=sums_view[:, :, cols], in0=firsts[:], in1=seconds[:], op=op)

        def vector_planes(c):
            return [p for p in range(PLANES) if c < GPSIMD_FROM or p not in GPSIMD_PLANES]

        def start_a(c):
            for plane in vector_planes(c):
                first_terms = stream.tile([P, NX], F32, bufs=PLANES)
                nc.scalar.activation(
                    out=first_terms[:], in_=q_x[:, plane, HALF_X : 3 * HALF_X], func=ACT.Copy,
                    scale=kappa_re[:, c, plane : plane + 1],
                )
                terms_of[c, plane] = first_terms

        def finish_a(c):
            if c < GPSIMD_FROM:
                start_planes(c)
            for plane in vector_planes(c):
                g, t = divmod(plane, PACK)
                nc.vector.scalar_tensor_tensor(
                    out=planes_of[c][:, g, t, :].rearrange("p (s x) -> p s x", s=2),
                    in0=q_x[:, plane, :].rearrange("p (s x) -> p s x", s=2),
                    scalar=kappa_im[:, c, plane : plane + 1],
                    in1=terms_of[c, plane][:].unsqueeze(1).to_broadcast([P, 2, NX]),
                    op0=ALU.mult, op1=ALU.add,
                )

        def regroup_a(c, g):
            a_grouped = stream.tile([P, 2 * NX, PACK], BF16, tag="grouped", align_bytes=64, bufs=5)
            a_planes = planes_of[c][:, g]
            to_view, from_view = side_by_side(a_grouped[:, 0:NX], a_planes[:, :, 0:NX])
            nc.scalar.copy(out=to_view, in_=from_view)
            to_view, from_view = side_by_side(a_grouped[:, NX:], a_planes[:, :, NX:][:, :, ::-1])
            nc.scalar.copy(out=to_view, in_=from_view)
            grouped_of[c, g] = a_grouped

        def quantise_a(c, g):
            if g == 0:
                a_codes = coil_pool.tile([P, PASSES, 4, HALF_X], U32, align_bytes=64)
                a_scales = coil_pool.tile([P, PASSES, 4, HALF_X], U8, align_bytes=64)
                words_of[c] = (a_codes, a_scales)
            a_codes, a_scales = words_of[c]
            quantise(
                nc, grouped_of[c, g][:],
                a_codes[:, g].rearrange("p w x -> p (w x)"),
                a_scales[:, g].rearrange("p w x -> p (w x)"),
            )

        def whole_a(c):
            start_a(c)
            finish_a(c)
            for g in range(PASSES):
                regroup_a(c, g)
                quantise_a(c, g)

        def tensor_a(c, g, pool, tags):
            a_sums = [pool.tile([P, PACK, P], F32, name="a_sum_%d" % j, tag=tags[j]) for j in range(len(tags))]
            banks = range(len(tags))
            if g == 0:
                order = [(t, j) for t in range(PACK) for j in banks]
            else:
                order = [(t, j) for j in banks for t in range(PACK)]
            a_grouped = stream.tile([P, 2 * NX, PACK], BF16, tag="grouped", align_bytes=64, bufs=5)
            for t, j in order:
                plane = g * PACK + t
                for term, block in enumerate((1 + j % 2, j)):
                    nc.tensor.matmul(
                        out=a_sums[j][:, t, :], lhsT=diagonal[:, c, plane, term, :],
                        rhs=q_x[:, plane, block * HALF_X : (block + 1) * HALF_X],
                        start=(t == 0 and term == 0), stop=(t == PACK - 1 and term == 1),
                    )
                if t == PACK - 1:
                    block = (RE_HIGH, IM_HIGH, RE_LOW, IM_LOW_NEG)[j]
                    from_view = a_sums[j][:].rearrange("p t x -> p x t")
                    if block in (RE_LOW, IM_LOW_NEG):
                        from_view = from_view[:, ::-1, :]
                    nc.scalar.copy(out=a_grouped[:, block * P : (block + 1) * P, :], in_=from_view)
            grouped_of[c, g] = a_grouped

        for c in range(TENSOR_COILS):
            tensor_a(c, 0, recon, ("recon_re", "recon_im", "recon_re", "recon_im"))
            tensor_a(c, 1, sums, ("combined_re_0", "combined_re_1", "combined_im_0", "combined_im_1"))

        quarter = keep.tile([P, 1], F32)
        nc.vector.tensor_scalar(
            out=quarter[:], in0=steps[:, 0:1], scalar1=0.0, scalar2=-0.25 * math.pi, op0=ALU.mult, op1=ALU.add
        )
        kappa_y = keep.tile([P, 2, PLANES, Y_COARSE], F32)
        nc.vector.tensor_tensor(
            out=kappa_y[:], in0=outer_factors[:, :, :, 0:Y_COARSE],
            in1=density_bf[:].rearrange("p o g t -> p o (g t)").unsqueeze(3).to_broadcast([P, 2, PLANES, Y_COARSE]),
            op=ALU.mult,
        )
        q_y = keep.tile([P, PLANES, 4 * FINE], F32)
        e_codes = keep.tile([P, PASSES, 3, NY], U32, align_bytes=64)
        e_scales = keep.tile([P, PASSES, 3, NY], U8, align_bytes=64)
        for g in range(PASSES):
            planes = slice(g * PACK, (g + 1) * PACK)
            sines_y = stream.tile([P, PACK, 2, FINE], F32, bufs=2)
            nc.scalar.activation(out=sines_y[:, :, 0, :], in_=fine_y[:, planes, :], func=ACT.Sin, scale=0.5)
            nc.scalar.activation(
                out=sines_y[:, :, 1, :], in_=fine_y[:, planes, :], func=ACT.Sin, bias=quarter[:], scale=0.5
            )
            squares_y = stream.tile([P, PACK, 2 * FINE], F32, bufs=2)
            nc.scalar.activation(out=squares_y[:], in_=sines_y[:].rearrange("p t w j -> p t (w j)"), func=ACT.Square)
            nc.vector.tensor_scalar(
                out=q_y[:, planes, FINE : 3 * FINE], in0=squares_y[:], scalar1=-1.0, scalar2=0.5,
                op0=ALU.mult, op1=ALU.add,
            )
            nc.vector.tensor_scalar(
                out=q_y[:, planes, 0:FINE], in0=squares_y[:, :, FINE:], scalar1=-0.5, scalar2=None, op0=ALU.add
            )
            nc.vector.tensor_scalar(
                out=q_y[:, planes, 3 * FINE :], in0=squares_y[:, :, 0:FINE], scalar1=-0.5, scalar2=None, op0=ALU.add
            )
            e_planes = stream.tile([P, PACK, Y_COARSE, 4 * FINE], BF16, bufs=2)
            for t in range(PACK):
                plane = g * PACK + t
                for n in range(Y_COARSE):
                    e_terms = stream.tile([P, 2 * FINE], F32, bufs=PACK * Y_COARSE)
                    nc.scalar.activation(
                        out=e_terms[:], in_=q_y[:, plane, FINE : 3 * FINE], func=ACT.Copy,
                        scale=kappa_y[:, 0, plane, n : n + 1],
                    )
                    nc.vector.scalar_tensor_tensor(
                        out=e_planes[:, t, n, :].rearrange("p (s j) -> p s j", s=2),
                        in0=q_y[:, plane, :].rearrange("p (s j) -> p s j", s=2),
                        scalar=kappa_y[:, 1, plane, n : n + 1],
                        in1=e_terms[:].unsqueeze(1).to_broadcast([P, 2, 2 * FINE]),
                        op0=ALU.mult, op1=ALU.add,
                    )
            e_grouped = [
                stream.tile([P, NY, PACK], BF16, name="e_grouped_%d" % kind, tag="grouped", align_bytes=64, bufs=5)
                for kind in (E_RE, E_IM, E_IM_NEG)
            ]
            for kind in (E_RE, E_IM):
                to_view = e_grouped[kind][:].rearrange("p (n h j) t -> p n h j t", n=Y_COARSE, h=2)
                blocks = e_planes[:].rearrange("p t n (b j) -> p n b j t", b=4)
                low = blocks[:, :, 2 + kind, ::-1, :]
                if kind == E_RE:
                    nc.scalar.copy(out=to_view[:, :, 1], in_=blocks[:, :, kind])
                    nc.scalar.copy(out=to_view[:, :, 0], in_=low)
                else:
                    nc.vector.tensor_copy(out=to_view[:, :, 1], in_=blocks[:, :, kind])
                    nc.vector.tensor_scalar(out=to_view[:, :, 0], in0=low, scalar1=-1.0, scalar2=None, op0=ALU.mult)
            nc.vector.memset(e_grouped[E_IM][:, 0:1, :], 0.0)
            nc.vector.tensor_scalar(
                out=e_grouped[E_IM_NEG][:], in0=e_grouped[E_IM][:], scalar1=-1.0, scalar2=None, op0=ALU.mult
            )
            if g == PASSES - 1:
                for c in range(TENSOR_COILS):
                    for a_pass in range(PASSES):
                        quantise_a(c, a_pass)
            for kind in (E_RE, E_IM, E_IM_NEG):
                quantise(nc, e_grouped[kind][:], e_codes[:, g, kind, :], e_scales[:, g, kind, :])
        table_change = keep.tile([P, 1], F32)
        nc.scalar.activation(out=table_change[:], in_=squares_y[:, PACK - 1, 0:1], func=ACT.Sqrt)

        combined_re = [sums.tile([P, NY], F32, name="combined_re_%d" % h) for h in range(X_TILES)]
        combined_im = [sums.tile([P, NY], F32, name="combined_im_%d" % h) for h in range(X_TILES)]
        def recon_matmuls(c, h):
            a_codes, a_scales = words_of[c]
            if h == 0:
                re_terms = ((RE_LOW, E_RE), (IM_LOW_NEG, E_IM))
                im_terms = ((RE_LOW, E_IM_NEG), (IM_LOW_NEG, E_RE))
            else:
                re_terms = ((RE_HIGH, E_RE), (IM_HIGH, E_IM_NEG))
                im_terms = ((RE_HIGH, E_IM), (IM_HIGH, E_RE))
            recon_re = recon.tile([P, NY], F32)
            recon_im = recon.tile([P, NY], F32)
            for acc, terms in ((recon_re, re_terms), (recon_im, im_terms)):
                for g in range(PASSES):
                    for i, (block, kind) in enumerate(terms):
                        nc.tensor.matmul_mx(
                            out=acc[:],
                            lhsT=a_codes[:, g, block, :].bitcast(FP8X4),
                            lhsT_scale=a_scales[:, g, block, :],
                            rhs=e_codes[:, g, kind, :].bitcast(FP8X4),
                            rhs_scale=e_scales[:, g, kind, :],
                            start=(g == 0 and i == 0),
                            stop=(g == PASSES - 1 and i == 1),
                        )
            return recon_re, recon_im

        def add_transposed(total, term, first, last):
            for j in range(Y_BLOCKS):
                cols = slice(j * P, (j + 1) * P)
                nc.tensor.matmul(
                    out=total[:, cols], lhsT=term[:, cols], rhs=identity[:], is_transpose=True,
                    start=(first and j == 0), stop=(last and j == Y_BLOCKS - 1),
                )

        def combine(c, h, recon_re, recon_im):
            s_re, s_im = maps_re[:, c, h, :], maps_im[:, c, h, :]
            first_coil, last_coil = c == 0, c == COILS - 1

            def times_s_im(out, factor, negated):
                if negated:
                    nc.vector.scalar_tensor_tensor(
                        out=out[:], in0=factor[:], scalar=-1.0, in1=s_im, op0=ALU.mult, op1=ALU.mult
                    )
                else:
                    nc.vector.tensor_tensor(out=out[:], in0=factor[:], in1=s_im, op=ALU.mult)

            re_s_re = stream.tile([P, NY], F32, bufs=2)
            nc.vector.tensor_tensor(out=re_s_re[:], in0=recon_re[:], in1=s_re, op=ALU.mult)
            add_transposed(combined_re[h], re_s_re, first_coil, False)
            re_s_im = stream.tile([P, NY], F32, bufs=2)
            times_s_im(re_s_im, recon_re, h == 1)
            add_transposed(combined_im[h], re_s_im, first_coil, False)
            im_s_im = stream.tile([P, NY], F32, bufs=2)
            times_s_im(im_s_im, recon_im, h == 0)
            add_transposed(combined_re[h], im_s_im, False, last_coil)
            im_s_re = stream.tile([P, NY], F32, bufs=2)
            nc.vector.tensor_tensor(out=im_s_re[:], in0=recon_im[:], in1=s_re, op=ALU.mult)
            add_transposed(combined_im[h], im_s_re, False, last_coil)

        early = []
        for c in range(COILS):
            making = c + AHEAD if c + AHEAD < COILS else None
            if making is not None:
                start_a(making)
            recons = early + [recon_matmuls(c, h) for h in range(len(early), X_TILES)]
            early = []
            if making is not None:
                finish_a(making)
                if making + 1 < COILS:
                    gpsimd_a(making + 1)
                for g in range(PASSES):
                    regroup_a(making, g)
            between = making == COILS - 1
            for half in range(X_TILES):
                combine(c, half, recons[half][0], recons[half][1])
                if making is not None and half == (0 if between else X_TILES - 1):
                    for g in range(PASSES):
                        quantise_a(making, g)
                if between and half == 0:
                    early = [recon_matmuls(making, 0)]

        out_rows = out.rearrange("b x y o -> (b x) (y o)")
        for h in range(X_TILES):
            for piece in range(2):
                power = recon.tile([P, NY // 2], F32, tag=("recon_re", "recon_im")[piece])
                cols = slice(piece * NY // 2, (piece + 1) * NY // 2)
                blocks = range(piece * Y_BLOCKS // 2, (piece + 1) * Y_BLOCKS // 2)
                squared = []
                for name, total in (("re_squared", combined_re[h]), ("im_squared", combined_im[h])):
                    square = ending.tile([P, NY // 2], F32, name=name, bufs=4)
                    nc.scalar.activation(out=square[:], in_=total[:, cols], func=ACT.Square)
                    squared.append(square)
                for i, square in enumerate(squared):
                    for n in range(len(blocks)):
                        nc.tensor.matmul(
                            out=power[:, n * P : (n + 1) * P], lhsT=square[:, n * P : (n + 1) * P], rhs=identity[:],
                            is_transpose=True, start=(i == 0 and n == 0), stop=(i == 1 and n == len(blocks) - 1),
                        )
                magnitude = ending.tile([P, NY // 2], F32, bufs=4)
                nc.scalar.activation(out=magnitude[:], in_=power[:], func=ACT.Sqrt)
                nc.sync.dma_start(out=out_rows[h * P : (h + 1) * P, cols], in_=magnitude[:])
